import numpy as np
import ml_dtypes


def mxq(x, axis, fmt="e4m3"):
    dtype, down = {"e4m3": (ml_dtypes.float8_e4m3fn, 7), "e5m2": (ml_dtypes.float8_e5m2, 14)}[fmt]
    v = np.moveaxis(np.asarray(x, np.float32).astype(ml_dtypes.bfloat16).astype(np.float64), axis, -1)
    blocks = v.reshape(v.shape[:-1] + (-1, 32))
    amax = np.abs(blocks).max(-1, keepdims=True)
    byte = np.maximum(np.where(amax > 0, np.frexp(amax)[1] - 1 + 127, 0) - down, 1)
    scale = np.exp2(byte - 127.0)
    codes = (blocks / scale).astype(np.float32).astype(dtype).astype(np.float64)
    return np.moveaxis((codes * scale).reshape(v.shape), -1, axis)


WIDE = False


def mx_kscale(k):
    if not WIDE:
        return np.ones(k)
    levels = np.array([10, -10, 5, -5, 0])
    if k % 512:
        return np.exp2(np.random.permutation(np.resize(levels, k // 32))).repeat(32)
    a = np.empty((k // 512, 16))
    for p in range(k // 512):
        a[p, :8] = np.random.permutation(np.resize(levels, 8))
        for g in range(8):
            far = levels[np.abs(levels - a[p, g]) >= 10]
            a[p, g + 8] = far[np.random.randint(len(far))]
    return np.exp2(a.ravel()).repeat(32)


BF16 = ml_dtypes.bfloat16


def bf(x):
    return np.asarray(x, np.float32).astype(BF16)


def f64(x):
    return np.asarray(x).astype(np.float64)


B, T, M, K, N, IN_MATS, OUT_MATS = 2, 256, 8, 16, 32, 32, 16
KC = IN_MATS * K
WID = OUT_MATS * N
IN_FEATURES = IN_MATS * M * K
OUT_FEATURES = OUT_MATS * M * N


def setup_inputs():
    s = mx_kscale(KC).reshape(IN_MATS, 1, K)
    x = np.random.standard_normal((B, T, IN_MATS, M, K)) * s
    weight = np.random.standard_normal((OUT_MATS, IN_MATS, N, K)) / np.sqrt(KC) / s
    bias = np.random.standard_normal((OUT_MATS, M, N)) * 0.3
    return {"x": bf(x.reshape(B, T, IN_FEATURES)), "weight": bf(weight), "bias": bf(bias)}


def core(x, weight, bias):
    Bc, Tc, _ = x.shape
    xb = f64(x).reshape(Bc, Tc, IN_MATS, M, K)
    xr = xb.transpose(0, 1, 3, 2, 4).reshape(Bc, Tc, M, KC)
    wr = f64(weight).transpose(0, 2, 1, 3).reshape(WID, KC)
    res = mxq(xr, 3, "e4m3") @ mxq(wr, 1, "e4m3").T
    res = res.reshape(Bc, Tc, M, OUT_MATS, N).transpose(0, 1, 3, 2, 4)
    res = res + f64(bias)
    return res.reshape(Bc, Tc, OUT_FEATURES)


def e4m3fn_bytes(y):
    return np.clip(np.asarray(y, np.float64), -448.0, 448.0).astype(np.float32).astype(ml_dtypes.float8_e4m3fn).view(np.uint8)


Y_SCALE = 210.0


def reference(x, weight, bias):
    out = core(x, weight, bias)
    return out, e4m3fn_bytes(out * Y_SCALE)

@@ -1,0 +1,272 @@
+from contextlib import ExitStack
+
+import concourse.mybir as mybir
+from concourse.masks import make_identity
+
+F32 = mybir.dt.float32
+BF16 = mybir.dt.bfloat16
+U32 = mybir.dt.uint32
+U8 = mybir.dt.uint8
+FP8X4 = mybir.dt.float8_e4m3fn_x4
+FP8 = mybir.dt.float8_e4m3fn
+ACT = mybir.ActivationFunctionType
+ALU = mybir.AluOpType
+
+P = 128
+TOKENS = 512
+FEATURES = 4096
+N_TILES = TOKENS // P
+Y_SCALE = 210.0
+HALF = 2048
+
+FLOPS = 2 * 4096 * 512 * 512
+
+
+def tile_blocklinear_kernel(tc, x, weight, bias, out_0, out_1):
+    nc = tc.nc
+    x_rows = x.flatten_outer_dims()
+    y_rows = out_0.flatten_outer_dims()
+    y8_rows = out_1.flatten_outer_dims()
+
+    with ExitStack() as ctx:
+        const = ctx.enter_context(tc.tile_pool(name="const", bufs=1))
+        xin = ctx.enter_context(tc.tile_pool(name="xin", bufs=N_TILES))
+        prep = ctx.enter_context(tc.tile_pool(name="prep", bufs=2))
+        outp = ctx.enter_context(tc.tile_pool(name="outp", bufs=5))
+        psum_t = ctx.enter_context(tc.psum_pool(name="psum_t", bufs=4))
+        psum_o = ctx.enter_context(tc.psum_pool(name="psum_o", bufs=4))
+        ctx.enter_context(tc.manual_schedule())
+
+        seed = const.tile([P, 1], F32, name="seed")
+        seed_out = const.tile([P, 1], F32, name="seed_out")
+        zb_lo = const.tile([P, HALF], BF16, name="zb_lo")
+        zb_hi = const.tile([P, HALF], BF16, name="zb_hi")
+        zb = [zb_lo, zb_hi]
+        ones = const.tile([P, P], BF16, name="ones")
+        ident = const.tile([P, P], F32, name="ident")
+        bias_sb = const.tile([P, FEATURES], BF16, name="bias_sb")
+        w_raw = const.tile([P, 2048], BF16, name="w_raw")
+        w_ord = const.tile([P, 2048], BF16, name="w_ord", align_bytes=64)
+        w_grp = const.tile([P, 2048], BF16, name="w_grp", align_bytes=64)
+        w_codes = const.tile([P, 512], U32, name="w_codes", align_bytes=64)
+        w_scales = const.tile([P, 512], U8, name="w_scales", align_bytes=64)
+
+        nc.vector.memset(seed[:], 0.0)
+        nc.scalar.activation(out=seed_out[:], in_=seed[:], func=ACT.Copy, scale=1.0)
+        nc.vector.memset(zb[0][:].bitcast(F32), 0.0)
+        nc.vector.memset(ones[:], 1.0)
+        nc.vector.memset(zb[1][:].bitcast(F32), 0.0)
+        make_identity(nc, ident[:])
+
+        bias_row = bias.rearrange("(u o) m n -> u (o m n)", u=1)
+        nc.scalar.dma_start(out=zb[0][0:1, :], in_=bias_row[:, 0:HALF])
+        x_raw = []
+        for i in range(N_TILES):
+            xt = xin.tile([P, FEATURES], BF16, name="x_raw%d" % i, tag="x_raw")
+            x_raw.append(xt)
+        for q in range(2):
+            nc.sync.dma_start(out=x_raw[0][:, q * HALF : (q + 1) * HALF], in_=x_rows[0:P, q * HALF : (q + 1) * HALF])
+        w_view = weight.rearrange("o (i par) (ng mm) k -> ng par o i (mm k)", par=2, ng=4, mm=8)
+        for s in range(8):
+            nc.sync.dma_start(
+                out=w_raw[s:P:8, :].rearrange("p (i f) -> p i f", i=16),
+                in_=w_view[s // 2, s % 2],
+            )
+        nc.scalar.dma_start(out=zb[1][0:1, :], in_=bias_row[:, HALF:FEATURES])
+        for i in range(1, N_TILES):
+            nc.sync.dma_start(out=x_raw[i][:], in_=x_rows[i * P : (i + 1) * P, :])
+
+        def spread_bias(q):
+            bp = psum_t.tile([P, 1024], BF16, name="bp", tag="tp")
+            for s in range(2):
+                c0 = (q % 2) * 1024 + s * 512
+                nc.tensor.matmul(
+                    out=bp[:, s * 512 : (s + 1) * 512],
+                    lhsT=ones[:],
+                    rhs=zb[q // 2][:, c0 : c0 + 512],
+                    start=True,
+                    stop=True,
+                )
+            nc.scalar.copy(out=bias_sb[:, q * 1024 : (q + 1) * 1024], in_=bp[:])
+
+        state = {}
+
+        def new_prep(i):
+            state["ord%d" % i] = prep.tile([P, FEATURES], BF16, name="x_ord", tag="x_ord", align_bytes=64)
+            state["grp%d" % i] = prep.tile([P, FEATURES], BF16, name="x_grp", tag="x_grp", align_bytes=64)
+            state["codes%d" % i] = prep.tile([P, 1024], U32, name="x_codes", tag="x_codes", align_bytes=64)
+            state["scales%d" % i] = prep.tile([P, 1024], U8, name="x_scales", tag="x_scales", align_bytes=64)
+
+        def reorder(i, par, m0, m1, i0, i1):
+            src = x_raw[i][:].rearrange("p (i par m k) -> p par m i k", par=2, m=8, k=16)
+            dst = state["ord%d" % i][:].rearrange("p (m par i k) -> p par m i k", m=8, par=2, k=16)
+            nc.vector.tensor_copy(out=dst[:, par, m0:m1, i0:i1, :], in_=src[:, par, m0:m1, i0:i1, :])
+
+        def turn(i, g):
+            tp = psum_t.tile([P, 512], F32, name="tp", tag="tp")
+            words = state["ord%d" % i][:].bitcast(F32)
+            for s in range(4):
+                blk = 4 * g + s
+                nc.tensor.transpose(tp[:, s * P : (s + 1) * P], words[:, blk * P : (blk + 1) * P], ident[:])
+            state["tp%d_%d" % (i, g)] = tp
+
+        def gather(i, g, on_vector):
+            tp = state["tp%d_%d" % (i, g)]
+            dst = state["grp%d" % i][:].bitcast(F32)[:, g * 512 : (g + 1) * 512]
+            dst = dst.rearrange("p (m t par) -> p m t par", m=2, par=2)
+            src = tp[:].rearrange("p (m par t) -> p m t par", m=2, par=2)
+            if on_vector:
+                nc.vector.tensor_copy(out=dst, in_=src)
+            else:
+                nc.scalar.copy(out=dst, in_=src)
+
+        def quantize(i, gg):
+            nc.vector.quantize_mx(
+                out=state["codes%d" % i][:, gg * 512 : (gg + 1) * 512].bitcast(FP8X4),
+                scales=state["scales%d" % i][:, gg * 512 : (gg + 1) * 512],
+                in_=state["grp%d" % i][:, gg * 2048 : (gg + 1) * 2048],
+            )
+
+        def multiply(i, o0, n_o, b):
+            width = 32 * n_o
+            per_bank = 512 // width
+            acc = psum_o.tile([P, 512], F32, name="acc", tag="acc")
+            for mm in range(per_bank):
+                m = b * per_bank + mm
+                nc.tensor.matmul_mx(
+                    out=acc[:, mm * width : (mm + 1) * width],
+                    lhsT=state["codes%d" % i][:, m * P : (m + 1) * P].bitcast(FP8X4),
+                    lhsT_scale=state["scales%d" % i][:, m * P : (m + 1) * P],
+                    rhs=w_codes[:, o0 * 32 : o0 * 32 + width].bitcast(FP8X4),
+                    rhs_scale=w_scales[:, o0 * 32 : o0 * 32 + width],
+                    start=True,
+                    stop=True,
+                )
+            state["acc%d_%d" % (o0, b)] = acc
+
+        def new_y(o0, n_o):
+            state["y%d" % o0] = outp.tile([P, n_o * 256], F32, name="y", tag="y")
+            state["z%d" % o0] = outp.tile([P, n_o * 256], FP8, name="y8", tag="y8")
+
+        def add_bias(o0, n_o, b):
+            per_bank = 16 // n_o
+            ms = slice(b * per_bank, (b + 1) * per_bank)
+            nc.vector.tensor_tensor(
+                out=state["y%d" % o0][:].rearrange("p (o m n) -> p o m n", o=n_o, m=8)[:, :, ms, :],
+                in0=state["acc%d_%d" % (o0, b)][:].rearrange("p (m o n) -> p o m n", m=per_bank, o=n_o),
+                in1=bias_sb[:].rearrange("p (o m n) -> p o m n", o=16, m=8)[:, o0 : o0 + n_o, ms, :],
+                op=ALU.add,
+            )
+
+        def store_y(i, o0, n_o):
+            nc.sync.dma_start(
+                out=y_rows[i * P : (i + 1) * P, o0 * 256 : (o0 + n_o) * 256], in_=state["y%d" % o0][:]
+            )
+
+        def cast(o0, c0, c1, on_vector):
+            y = state["y%d" % o0]
+            y8 = state["z%d" % o0]
+            if on_vector:
+                nc.vector.tensor_scalar(
+                    out=y8[:, c0:c1], in0=y[:, c0:c1], scalar1=Y_SCALE, scalar2=None, op0=ALU.mult, saturate=False
+                )
+            else:
+                nc.scalar.activation(out=y8[:, c0:c1], in_=y[:, c0:c1], func=ACT.Copy, scale=Y_SCALE, saturate=False)
+
+        def store_y8(i, o0, n_o):
+            nc.sync.dma_start(
+                out=y8_rows[i * P : (i + 1) * P, o0 * 256 : (o0 + n_o) * 256],
+                in_=state["z%d" % o0][:].bitcast(U8),
+            )
+
+        spread_bias(0)
+        spread_bias(1)
+        new_prep(0)
+        for q in range(2):
+            for par in range(2):
+                reorder(0, par, 0, 8, 8 * q, 8 * q + 8)
+        for g in range(4):
+            turn(0, g)
+        gather(0, 0, False)
+        gather(0, 1, False)
+
+        w_src = w_raw[:].rearrange("p (i mm k) -> p mm i k", i=16, mm=8)
+        w_dst = w_ord[:].rearrange("p (mm i k) -> p mm i k", mm=8, i=16)
+        w_words = w_ord[:].bitcast(F32)
+        w_grp_view = w_grp[:].bitcast(F32).rearrange("p (q mm par) -> p q mm par", mm=8, par=2)
+        for bank in range(2):
+            nc.vector.tensor_copy(out=w_dst[:, 4 * bank : 4 * bank + 4], in_=w_src[:, 4 * bank : 4 * bank + 4])
+        quantize(0, 0)
+        for bank in range(2):
+            tw = psum_t.tile([P, 512], F32, name="tw", tag="tp")
+            for s in range(4):
+                mm = 4 * bank + s
+                nc.tensor.transpose(tw[:, s * P : (s + 1) * P], w_words[:, mm * P : (mm + 1) * P], ident[:])
+            tw_view = tw[:].rearrange("p (mm q par) -> p q mm par", mm=4, par=2)
+            if bank == 0:
+                nc.scalar.copy(out=w_grp_view[:, :, 0:4, :], in_=tw_view)
+            else:
+                nc.vector.tensor_copy(out=w_grp_view[:, :, 4:8, :], in_=tw_view)
+        nc.vector.quantize_mx(out=w_codes[:].bitcast(FP8X4), scales=w_scales[:], in_=w_grp[:])
+        gather(0, 2, False)
+        gather(0, 3, False)
+        quantize(0, 1)
+
+        for i in range(N_TILES):
+            nxt = i + 1 < N_TILES
+            for b in range(4):
+                multiply(i, 0, 8, b)
+            if i == 0:
+                spread_bias(2)
+                spread_bias(3)
+            if nxt:
+                new_prep(i + 1)
+                for par in range(2):
+                    reorder(i + 1, par, 0, 8, 0, 16)
+                for g in range(4):
+                    turn(i + 1, g)
+            new_y(0, 8)
+            for b in range(4):
+                add_bias(0, 8, b)
+            store_y(i, 0, 8)
+            if nxt:
+                for g in range(4):
+                    gather(i + 1, g, False)
+            cast(0, 0, HALF, False)
+            if nxt:
+                store_y8(i, 0, 8)
+                for b in range(4):
+                    multiply(i, 8, 8, b)
+                new_y(8, 8)
+                add_bias(8, 8, 0)
+                add_bias(8, 8, 1)
+                quantize(i + 1, 0)
+                add_bias(8, 8, 2)
+                add_bias(8, 8, 3)
+                store_y(i, 8, 8)
+                quantize(i + 1, 1)
+                cast(8, 0, HALF, False)
+                store_y8(i, 8, 8)
+            else:
+                multiply(i, 8, 4, 0)
+                multiply(i, 8, 4, 1)
+                multiply(i, 12, 2, 0)
+                multiply(i, 14, 2, 0)
+                new_y(8, 4)
+                add_bias(8, 4, 0)
+                add_bias(8, 4, 1)
+                store_y(i, 8, 4)
+                cast(8, 256, 1024, False)
+                new_y(12, 2)
+                add_bias(12, 2, 0)
+                store_y(i, 12, 2)
+                new_y(14, 2)
+                add_bias(14, 2, 0)
+                store_y(i, 14, 2)
+                store_y8(i, 0, 8)
+                cast(8, 0, 256, True)
+                store_y8(i, 8, 4)
+                cast(12, 0, 512, True)
+                store_y8(i, 12, 2)
+                cast(14, 0, 512, True)
+                store_y8(i, 14, 2)

@@ -39,10 +39,6 @@ def tile_blocklinear_kernel(tc, x, weight, bias, out_0, out_1):
 
         seed = const.tile([P, 1], F32, name="seed")
         seed_out = const.tile([P, 1], F32, name="seed_out")
-        zb_lo = const.tile([P, HALF], BF16, name="zb_lo")
-        zb_hi = const.tile([P, HALF], BF16, name="zb_hi")
-        zb = [zb_lo, zb_hi]
-        ones = const.tile([P, P], BF16, name="ones")
         ident = const.tile([P, P], F32, name="ident")
         bias_sb = const.tile([P, FEATURES], BF16, name="bias_sb")
         w_raw = const.tile([P, 2048], BF16, name="w_raw")
@@ -53,13 +49,8 @@ def tile_blocklinear_kernel(tc, x, weight, bias, out_0, out_1):
 
         nc.vector.memset(seed[:], 0.0)
         nc.scalar.activation(out=seed_out[:], in_=seed[:], func=ACT.Copy, scale=1.0)
-        nc.vector.memset(zb[0][:].bitcast(F32), 0.0)
-        nc.vector.memset(ones[:], 1.0)
-        nc.vector.memset(zb[1][:].bitcast(F32), 0.0)
         make_identity(nc, ident[:])
 
-        bias_row = bias.rearrange("(u o) m n -> u (o m n)", u=1)
-        nc.scalar.dma_start(out=zb[0][0:1, :], in_=bias_row[:, 0:HALF])
         x_raw = []
         for i in range(N_TILES):
             xt = xin.tile([P, FEATURES], BF16, name="x_raw%d" % i, tag="x_raw")
@@ -72,22 +63,9 @@ def tile_blocklinear_kernel(tc, x, weight, bias, out_0, out_1):
                 out=w_raw[s:P:8, :].rearrange("p (i f) -> p i f", i=16),
                 in_=w_view[s // 2, s % 2],
             )
-        nc.scalar.dma_start(out=zb[1][0:1, :], in_=bias_row[:, HALF:FEATURES])
+        nc.sync.dma_start(out=bias_sb[:], in_=bias.rearrange("o m n -> (o m n)").partition_broadcast(P))
         for i in range(1, N_TILES):
             nc.sync.dma_start(out=x_raw[i][:], in_=x_rows[i * P : (i + 1) * P, :])
-
-        def spread_bias(q):
-            bp = psum_t.tile([P, 1024], BF16, name="bp", tag="tp")
-            for s in range(2):
-                c0 = (q % 2) * 1024 + s * 512
-                nc.tensor.matmul(
-                    out=bp[:, s * 512 : (s + 1) * 512],
-                    lhsT=ones[:],
-                    rhs=zb[q // 2][:, c0 : c0 + 512],
-                    start=True,
-                    stop=True,
-                )
-            nc.scalar.copy(out=bias_sb[:, q * 1024 : (q + 1) * 1024], in_=bp[:])
 
         state = {}
 
@@ -179,8 +157,6 @@ def tile_blocklinear_kernel(tc, x, weight, bias, out_0, out_1):
                 in_=state["z%d" % o0][:].bitcast(U8),
             )
 
-        spread_bias(0)
-        spread_bias(1)
         new_prep(0)
         for q in range(2):
             for par in range(2):
@@ -216,9 +192,6 @@ def tile_blocklinear_kernel(tc, x, weight, bias, out_0, out_1):
             nxt = i + 1 < N_TILES
             for b in range(4):
                 multiply(i, 0, 8, b)
-            if i == 0:
-                spread_bias(2)
-                spread_bias(3)
             if nxt:
                 new_prep(i + 1)
                 for par in range(2):

@@ -63,8 +63,11 @@ def tile_blocklinear_kernel(tc, x, weight, bias, out_0, out_1):
                 out=w_raw[s:P:8, :].rearrange("p (i f) -> p i f", i=16),
                 in_=w_view[s // 2, s % 2],
             )
-        nc.sync.dma_start(out=bias_sb[:], in_=bias.rearrange("o m n -> (o m n)").partition_broadcast(P))
-        for i in range(1, N_TILES):
+        nc.sync.dma_start(out=x_raw[1][:], in_=x_rows[P : 2 * P, :])
+        bias_flat = bias.rearrange("o m n -> (o m n)")
+        nc.sync.dma_start(out=bias_sb[:, 0:HALF], in_=bias_flat[0:HALF].partition_broadcast(P))
+        nc.sync.dma_start(out=bias_sb[:, HALF:FEATURES], in_=bias_flat[HALF:FEATURES].partition_broadcast(P))
+        for i in range(2, N_TILES):
             nc.sync.dma_start(out=x_raw[i][:], in_=x_rows[i * P : (i + 1) * P, :])
 
         state = {}

@@ -55,10 +55,13 @@ def tile_blocklinear_kernel(tc, x, weight, bias, out_0, out_1):
         for i in range(N_TILES):
             xt = xin.tile([P, FEATURES], BF16, name="x_raw%d" % i, tag="x_raw")
             x_raw.append(xt)
-        for q in range(2):
-            nc.sync.dma_start(out=x_raw[0][:, q * HALF : (q + 1) * HALF], in_=x_rows[0:P, q * HALF : (q + 1) * HALF])
         w_view = weight.rearrange("o (i par) (ng mm) k -> ng par o i (mm k)", par=2, ng=4, mm=8)
         for s in range(8):
+            if s == 2:
+                for q in range(2):
+                    nc.sync.dma_start(
+                        out=x_raw[0][:, q * HALF : (q + 1) * HALF], in_=x_rows[0:P, q * HALF : (q + 1) * HALF]
+                    )
             nc.sync.dma_start(
                 out=w_raw[s:P:8, :].rearrange("p (i f) -> p i f", i=16),
                 in_=w_view[s // 2, s % 2],
@@ -81,7 +84,12 @@ def tile_blocklinear_kernel(tc, x, weight, bias, out_0, out_1):
         def reorder(i, par, m0, m1, i0, i1):
             src = x_raw[i][:].rearrange("p (i par m k) -> p par m i k", par=2, m=8, k=16)
             dst = state["ord%d" % i][:].rearrange("p (m par i k) -> p par m i k", m=8, par=2, k=16)
-            nc.vector.tensor_copy(out=dst[:, par, m0:m1, i0:i1, :], in_=src[:, par, m0:m1, i0:i1, :])
+            if i == 1:
+                src = x_raw[i][:].bitcast(F32).rearrange("p (i par m kk) -> p par m i kk", par=2, m=8, kk=8)
+                dst = state["ord%d" % i][:].bitcast(F32).rearrange("p (m par i kk) -> p par m i kk", m=8, par=2, kk=8)
+                nc.scalar.copy(out=dst[:, par, m0:m1, i0:i1, :], in_=src[:, par, m0:m1, i0:i1, :])
+            else:
+                nc.vector.tensor_copy(out=dst[:, par, m0:m1, i0:i1, :], in_=src[:, par, m0:m1, i0:i1, :])
 
         def turn(i, g):
             tp = psum_t.tile([P, 512], F32, name="tp", tag="tp")

@@ -18,6 +18,9 @@ FEATURES = 4096
 N_TILES = TOKENS // P
 Y_SCALE = 210.0
 HALF = 2048
+N_WARM = 4
+N_S_BEFORE = 6
+TAIL_ON_V = [True, True, False, True, True, False, True, True, False, True, True]
 
 FLOPS = 2 * 4096 * 512 * 512
 
@@ -32,7 +35,9 @@ def tile_blocklinear_kernel(tc, x, weight, bias, out_0, out_1):
         const = ctx.enter_context(tc.tile_pool(name="const", bufs=1))
         xin = ctx.enter_context(tc.tile_pool(name="xin", bufs=N_TILES))
         prep = ctx.enter_context(tc.tile_pool(name="prep", bufs=2))
-        outp = ctx.enter_context(tc.tile_pool(name="outp", bufs=5))
+        ordp = ctx.enter_context(tc.tile_pool(name="ordp", bufs=4))
+        outp = ctx.enter_context(tc.tile_pool(name="outp", bufs=8))
+        out8 = ctx.enter_context(tc.tile_pool(name="out8", bufs=8))
         psum_t = ctx.enter_context(tc.psum_pool(name="psum_t", bufs=4))
         psum_o = ctx.enter_context(tc.psum_pool(name="psum_o", bufs=4))
         ctx.enter_context(tc.manual_schedule())
@@ -40,6 +45,9 @@ def tile_blocklinear_kernel(tc, x, weight, bias, out_0, out_1):
         seed = const.tile([P, 1], F32, name="seed")
         seed_out = const.tile([P, 1], F32, name="seed_out")
         ident = const.tile([P, P], F32, name="ident")
+        ident_bf = const.tile([P, P], BF16, name="ident_bf")
+        warm = const.tile([P, 512], BF16, name="warm")
+        bias_rows = const.tile([P, 512], BF16, name="bias_rows")
         bias_sb = const.tile([P, FEATURES], BF16, name="bias_sb")
         w_raw = const.tile([P, 2048], BF16, name="w_raw")
         w_ord = const.tile([P, 2048], BF16, name="w_ord", align_bytes=64)
@@ -47,8 +55,11 @@ def tile_blocklinear_kernel(tc, x, weight, bias, out_0, out_1):
         w_codes = const.tile([P, 512], U32, name="w_codes", align_bytes=64)
         w_scales = const.tile([P, 512], U8, name="w_scales", align_bytes=64)
 
+        nc.vector.memset(bias_rows[:], 0.0)
+        nc.vector.memset(warm[:], 0.0)
         nc.vector.memset(seed[:], 0.0)
         nc.scalar.activation(out=seed_out[:], in_=seed[:], func=ACT.Copy, scale=1.0)
+        make_identity(nc, ident_bf[:])
         make_identity(nc, ident[:])
 
         x_raw = []
@@ -56,39 +67,60 @@ def tile_blocklinear_kernel(tc, x, weight, bias, out_0, out_1):
             xt = xin.tile([P, FEATURES], BF16, name="x_raw%d" % i, tag="x_raw")
             x_raw.append(xt)
         w_view = weight.rearrange("o (i par) (ng mm) k -> ng par o i (mm k)", par=2, ng=4, mm=8)
-        for s in range(8):
-            if s == 2:
-                for q in range(2):
-                    nc.sync.dma_start(
-                        out=x_raw[0][:, q * HALF : (q + 1) * HALF], in_=x_rows[0:P, q * HALF : (q + 1) * HALF]
-                    )
-            nc.sync.dma_start(
-                out=w_raw[s:P:8, :].rearrange("p (i f) -> p i f", i=16),
-                in_=w_view[s // 2, s % 2],
-            )
-        nc.sync.dma_start(out=x_raw[1][:], in_=x_rows[P : 2 * P, :])
         bias_flat = bias.rearrange("o m n -> (o m n)")
-        nc.sync.dma_start(out=bias_sb[:, 0:HALF], in_=bias_flat[0:HALF].partition_broadcast(P))
-        nc.sync.dma_start(out=bias_sb[:, HALF:FEATURES], in_=bias_flat[HALF:FEATURES].partition_broadcast(P))
-        for i in range(2, N_TILES):
+
+        def load_w(s):
+            nc.sync.dma_start(out=w_raw[s:P:8, :].rearrange("p (i f) -> p i f", i=16), in_=w_view[s // 2, s % 2])
+
+        def load_x0(q):
+            nc.sync.dma_start(out=x_raw[0][:, q * HALF : (q + 1) * HALF], in_=x_rows[0:P, q * HALF : (q + 1) * HALF])
+
+        def load_bias():
+            nc.sync.dma_start(out=bias_rows[0:8, :], in_=bias_flat.rearrange("(g c) -> g c", g=8))
+
+        load_w(0)
+        load_w(1)
+        load_bias()
+        for s in range(2, 6):
+            load_w(s)
+        load_x0(0)
+        load_w(6)
+        load_w(7)
+        load_x0(1)
+        for i in range(1, N_TILES):
             nc.sync.dma_start(out=x_raw[i][:], in_=x_rows[i * P : (i + 1) * P, :])
 
         state = {}
 
+        def new_ord(i):
+            state["ord%d" % i] = ordp.tile([P, FEATURES], BF16, name="x_ord", tag="x_ord", align_bytes=64)
+
         def new_prep(i):
-            state["ord%d" % i] = prep.tile([P, FEATURES], BF16, name="x_ord", tag="x_ord", align_bytes=64)
+            if "ord%d" % i not in state:
+                new_ord(i)
             state["grp%d" % i] = prep.tile([P, FEATURES], BF16, name="x_grp", tag="x_grp", align_bytes=64)
             state["codes%d" % i] = prep.tile([P, 1024], U32, name="x_codes", tag="x_codes", align_bytes=64)
             state["scales%d" % i] = prep.tile([P, 1024], U8, name="x_scales", tag="x_scales", align_bytes=64)
 
-        def reorder(i, par, m0, m1, i0, i1):
-            src = x_raw[i][:].rearrange("p (i par m k) -> p par m i k", par=2, m=8, k=16)
-            dst = state["ord%d" % i][:].rearrange("p (m par i k) -> p par m i k", m=8, par=2, k=16)
-            if i == 1:
+        def reorder(i, par, m0, m1, i0, i1, on_scalar=False, on_gpsimd=False):
+            if on_gpsimd:
+                src = x_raw[i][:].rearrange("p (i par m k) -> p par m i k", par=2, m=8, k=16)
+                dst = state["ord%d" % i][:].rearrange("p (m par i k) -> p par m i k", m=8, par=2, k=16)
+                nc.gpsimd.tensor_scalar(
+                    out=dst[:, par, m0:m1, i0:i1, :],
+                    in0=src[:, par, m0:m1, i0:i1, :],
+                    scalar1=1.0,
+                    scalar2=0.0,
+                    op0=ALU.mult,
+                    op1=ALU.add,
+                )
+            elif on_scalar:
                 src = x_raw[i][:].bitcast(F32).rearrange("p (i par m kk) -> p par m i kk", par=2, m=8, kk=8)
                 dst = state["ord%d" % i][:].bitcast(F32).rearrange("p (m par i kk) -> p par m i kk", m=8, par=2, kk=8)
                 nc.scalar.copy(out=dst[:, par, m0:m1, i0:i1, :], in_=src[:, par, m0:m1, i0:i1, :])
             else:
+                src = x_raw[i][:].rearrange("p (i par m k) -> p par m i k", par=2, m=8, k=16)
+                dst = state["ord%d" % i][:].rearrange("p (m par i k) -> p par m i k", m=8, par=2, k=16)
                 nc.vector.tensor_copy(out=dst[:, par, m0:m1, i0:i1, :], in_=src[:, par, m0:m1, i0:i1, :])
 
         def turn(i, g):
@@ -109,11 +141,11 @@ def tile_blocklinear_kernel(tc, x, weight, bias, out_0, out_1):
             else:
                 nc.scalar.copy(out=dst, in_=src)
 
-        def quantize(i, gg):
+        def quantize(i, g0, g1):
             nc.vector.quantize_mx(
-                out=state["codes%d" % i][:, gg * 512 : (gg + 1) * 512].bitcast(FP8X4),
-                scales=state["scales%d" % i][:, gg * 512 : (gg + 1) * 512],
-                in_=state["grp%d" % i][:, gg * 2048 : (gg + 1) * 2048],
+                out=state["codes%d" % i][:, g0 * 256 : g1 * 256].bitcast(FP8X4),
+                scales=state["scales%d" % i][:, g0 * 256 : g1 * 256],
+                in_=state["grp%d" % i][:, g0 * 1024 : g1 * 1024],
             )
 
         def multiply(i, o0, n_o, b):
@@ -133,15 +165,17 @@ def tile_blocklinear_kernel(tc, x, weight, bias, out_0, out_1):
                 )
             state["acc%d_%d" % (o0, b)] = acc
 
-        def new_y(o0, n_o):
-            state["y%d" % o0] = outp.tile([P, n_o * 256], F32, name="y", tag="y")
-            state["z%d" % o0] = outp.tile([P, n_o * 256], FP8, name="y8", tag="y8")
+        def new_y(i, o0, n_o):
+            state["y%d_%d" % (i, o0)] = outp.tile([P, n_o * 256], F32, name="y", tag="y")
 
-        def add_bias(o0, n_o, b):
+        def new_y8(i, o0, n_o):
+            state["z%d_%d" % (i, o0)] = out8.tile([P, n_o * 256], FP8, name="y8", tag="y8")
+
+        def add_bias(i, o0, n_o, b):
             per_bank = 16 // n_o
             ms = slice(b * per_bank, (b + 1) * per_bank)
             nc.vector.tensor_tensor(
-                out=state["y%d" % o0][:].rearrange("p (o m n) -> p o m n", o=n_o, m=8)[:, :, ms, :],
+                out=state["y%d_%d" % (i, o0)][:].rearrange("p (o m n) -> p o m n", o=n_o, m=8)[:, :, ms, :],
                 in0=state["acc%d_%d" % (o0, b)][:].rearrange("p (m o n) -> p o m n", m=per_bank, o=n_o),
                 in1=bias_sb[:].rearrange("p (o m n) -> p o m n", o=16, m=8)[:, o0 : o0 + n_o, ms, :],
                 op=ALU.add,
@@ -149,12 +183,12 @@ def tile_blocklinear_kernel(tc, x, weight, bias, out_0, out_1):
 
         def store_y(i, o0, n_o):
             nc.sync.dma_start(
-                out=y_rows[i * P : (i + 1) * P, o0 * 256 : (o0 + n_o) * 256], in_=state["y%d" % o0][:]
+                out=y_rows[i * P : (i + 1) * P, o0 * 256 : (o0 + n_o) * 256], in_=state["y%d_%d" % (i, o0)][:]
             )
 
-        def cast(o0, c0, c1, on_vector):
-            y = state["y%d" % o0]
-            y8 = state["z%d" % o0]
+        def cast(i, o0, c0, c1, on_vector):
+            y = state["y%d_%d" % (i, o0)]
+            y8 = state["z%d_%d" % (i, o0)]
             if on_vector:
                 nc.vector.tensor_scalar(
                     out=y8[:, c0:c1], in0=y[:, c0:c1], scalar1=Y_SCALE, scalar2=None, op0=ALU.mult, saturate=False
@@ -165,92 +199,150 @@ def tile_blocklinear_kernel(tc, x, weight, bias, out_0, out_1):
         def store_y8(i, o0, n_o):
             nc.sync.dma_start(
                 out=y8_rows[i * P : (i + 1) * P, o0 * 256 : (o0 + n_o) * 256],
-                in_=state["z%d" % o0][:].bitcast(U8),
+                in_=state["z%d_%d" % (i, o0)][:].bitcast(U8),
             )
-
-        new_prep(0)
-        for q in range(2):
-            for par in range(2):
-                reorder(0, par, 0, 8, 8 * q, 8 * q + 8)
-        for g in range(4):
-            turn(0, g)
-        gather(0, 0, False)
-        gather(0, 1, False)
 
         w_src = w_raw[:].rearrange("p (i mm k) -> p mm i k", i=16, mm=8)
         w_dst = w_ord[:].rearrange("p (mm i k) -> p mm i k", mm=8, i=16)
         w_words = w_ord[:].bitcast(F32)
         w_grp_view = w_grp[:].bitcast(F32).rearrange("p (q mm par) -> p q mm par", mm=8, par=2)
-        for bank in range(2):
+
+        def w_reorder(bank):
             nc.vector.tensor_copy(out=w_dst[:, 4 * bank : 4 * bank + 4], in_=w_src[:, 4 * bank : 4 * bank + 4])
-        quantize(0, 0)
-        for bank in range(2):
+
+        def w_turn(bank):
             tw = psum_t.tile([P, 512], F32, name="tw", tag="tp")
             for s in range(4):
                 mm = 4 * bank + s
                 nc.tensor.transpose(tw[:, s * P : (s + 1) * P], w_words[:, mm * P : (mm + 1) * P], ident[:])
-            tw_view = tw[:].rearrange("p (mm q par) -> p q mm par", mm=4, par=2)
-            if bank == 0:
-                nc.scalar.copy(out=w_grp_view[:, :, 0:4, :], in_=tw_view)
+            state["tw%d" % bank] = tw
+
+        def w_gather(bank, on_vector):
+            tw_view = state["tw%d" % bank][:].rearrange("p (mm q par) -> p q mm par", mm=4, par=2)
+            if on_vector:
+                nc.vector.tensor_copy(out=w_grp_view[:, :, 4 * bank : 4 * bank + 4, :], in_=tw_view)
             else:
-                nc.vector.tensor_copy(out=w_grp_view[:, :, 4:8, :], in_=tw_view)
-        nc.vector.quantize_mx(out=w_codes[:].bitcast(FP8X4), scales=w_scales[:], in_=w_grp[:])
+                nc.scalar.copy(out=w_grp_view[:, :, 4 * bank : 4 * bank + 4, :], in_=tw_view)
+
+        def w_quantize():
+            nc.vector.quantize_mx(out=w_codes[:].bitcast(FP8X4), scales=w_scales[:], in_=w_grp[:])
+
+        for j in range(N_WARM):
+            pw = psum_t.tile([P, 512], F32, name="pw", tag="tp")
+            nc.tensor.matmul(out=pw[:], lhsT=warm[:, 0:P], rhs=warm[:], start=True, stop=True)
+        for j in range(4):
+            pb = psum_o.tile([P, 1024], BF16, name="pb", tag="acc")
+            for h in range(2):
+                g = 2 * j + h
+                nc.tensor.matmul(
+                    out=pb[:, h * 512 : (h + 1) * 512],
+                    lhsT=ident_bf[:, g : g + 1].to_broadcast([P, P]),
+                    rhs=bias_rows[:],
+                    start=True,
+                    stop=True,
+                )
+            if j % 2 == 0:
+                nc.vector.tensor_copy(out=bias_sb[:, j * 1024 : (j + 1) * 1024], in_=pb[:])
+            else:
+                nc.scalar.copy(out=bias_sb[:, j * 1024 : (j + 1) * 1024], in_=pb[:])
+        new_prep(0)
+        for par in range(2):
+            reorder(0, par, 0, 8, 0, 8)
+        for bank in range(2):
+            w_reorder(bank)
+            w_turn(bank)
+        for mh in range(2):
+            for par in range(2):
+                reorder(0, par, 4 * mh, 4 * mh + 4, 8, 16)
+        w_gather(0, False)
+        w_gather(1, False)
+        for g in range(4):
+            turn(0, g)
+        w_quantize()
+        new_y(0, 0, 8)
+        new_prep(1)
+        gather(0, 0, False)
+        quantize(0, 0, 1)
+        multiply(0, 0, 8, 0)
+        gather(0, 1, False)
+        quantize(0, 1, 2)
+        multiply(0, 0, 8, 1)
+        add_bias(0, 0, 8, 0)
         gather(0, 2, False)
+        quantize(0, 2, 3)
+        multiply(0, 0, 8, 2)
+        add_bias(0, 0, 8, 1)
         gather(0, 3, False)
-        quantize(0, 1)
+        quantize(0, 3, 4)
+        multiply(0, 0, 8, 3)
+        reorder(1, 0, 0, 8, 0, 16, True)
+        reorder(1, 1, 0, 8, 0, 16, True)
+        add_bias(0, 0, 8, 2)
+        add_bias(0, 0, 8, 3)
+        store_y(0, 0, 8)
+
+        todo = []
+        state["cast_done"] = 0
+
+        def cast_next(on_vector):
+            ci, co, c0, c1 = todo[state["cast_done"]]
+            state["cast_done"] = state["cast_done"] + 1
+            if c0 == 0:
+                new_y8(ci, co, 8)
+            cast(ci, co, c0, c1, on_vector)
+            if c1 == HALF:
+                store_y8(ci, co, 8)
 
         for i in range(N_TILES):
             nxt = i + 1 < N_TILES
-            for b in range(4):
-                multiply(i, 0, 8, b)
+            last = not nxt
+            if i > 0:
+                for b in range(4):
+                    multiply(i, 0, 8, b)
+                new_y(i, 0, 8)
+                add_bias(i, 0, 8, 0)
+                add_bias(i, 0, 8, 1)
+            if last:
+                cast_next(False)
+            multiply(i, 8, 8, 0)
+            multiply(i, 8, 8, 1)
             if nxt:
-                new_prep(i + 1)
-                for par in range(2):
-                    reorder(i + 1, par, 0, 8, 0, 16)
                 for g in range(4):
                     turn(i + 1, g)
-            new_y(0, 8)
-            for b in range(4):
-                add_bias(0, 8, b)
-            store_y(i, 0, 8)
+            if i > 0:
+                add_bias(i, 0, 8, 2)
+                add_bias(i, 0, 8, 3)
+                store_y(i, 0, 8)
+            if last:
+                cast_next(False)
+            multiply(i, 8, 8, 2)
+            multiply(i, 8, 8, 3)
+            todo.extend([(i, 0, 0, 1024), (i, 0, 1024, HALF)])
+            if i > 0 and nxt:
+                cast_next(False)
             if nxt:
                 for g in range(4):
                     gather(i + 1, g, False)
-            cast(0, 0, HALF, False)
+            new_y(i, 8, 8)
+            add_bias(i, 8, 8, 0)
+            add_bias(i, 8, 8, 1)
             if nxt:
-                store_y8(i, 0, 8)
-                for b in range(4):
-                    multiply(i, 8, 8, b)
-                new_y(8, 8)
-                add_bias(8, 8, 0)
-                add_bias(8, 8, 1)
-                quantize(i + 1, 0)
-                add_bias(8, 8, 2)
-                add_bias(8, 8, 3)
-                store_y(i, 8, 8)
-                quantize(i + 1, 1)
-                cast(8, 0, HALF, False)
-                store_y8(i, 8, 8)
-            else:
-                multiply(i, 8, 4, 0)
-                multiply(i, 8, 4, 1)
-                multiply(i, 12, 2, 0)
-                multiply(i, 14, 2, 0)
-                new_y(8, 4)
-                add_bias(8, 4, 0)
-                add_bias(8, 4, 1)
-                store_y(i, 8, 4)
-                cast(8, 256, 1024, False)
-                new_y(12, 2)
-                add_bias(12, 2, 0)
-                store_y(i, 12, 2)
-                new_y(14, 2)
-                add_bias(14, 2, 0)
-                store_y(i, 14, 2)
-                store_y8(i, 0, 8)
-                cast(8, 0, 256, True)
-                store_y8(i, 8, 4)
-                cast(12, 0, 512, True)
-                store_y8(i, 12, 2)
-                cast(14, 0, 512, True)
-                store_y8(i, 14, 2)
+                quantize(i + 1, 0, 2)
+            if last:
+                cast_next(False)
+            add_bias(i, 8, 8, 2)
+            add_bias(i, 8, 8, 3)
+            store_y(i, 8, 8)
+            todo.extend([(i, 8, 0, 1024), (i, 8, 1024, HALF)])
+            if nxt:
+                quantize(i + 1, 2, 4)
+            if last:
+                cast_next(False)
+            if i + 2 < N_TILES:
+                new_prep(i + 2)
+                for par in range(2):
+                    reorder(i + 2, par, 0, 8, 0, 16, True)
+            if i == 2:
+                cast_next(False)
+        for j in range(len(todo) - state["cast_done"]):
+            cast_next(TAIL_ON_V[j])

@@ -36,8 +36,9 @@ def tile_blocklinear_kernel(tc, x, weight, bias, out_0, out_1):
         xin = ctx.enter_context(tc.tile_pool(name="xin", bufs=N_TILES))
         prep = ctx.enter_context(tc.tile_pool(name="prep", bufs=2))
         ordp = ctx.enter_context(tc.tile_pool(name="ordp", bufs=4))
-        outp = ctx.enter_context(tc.tile_pool(name="outp", bufs=8))
-        out8 = ctx.enter_context(tc.tile_pool(name="out8", bufs=8))
+        rawp = ctx.enter_context(tc.tile_pool(name="rawp", bufs=3))
+        outp = ctx.enter_context(tc.tile_pool(name="outp", bufs=10))
+        out8 = ctx.enter_context(tc.tile_pool(name="out8", bufs=10))
         psum_t = ctx.enter_context(tc.psum_pool(name="psum_t", bufs=4))
         psum_o = ctx.enter_context(tc.psum_pool(name="psum_o", bufs=4))
         ctx.enter_context(tc.manual_schedule())
@@ -102,14 +103,14 @@ def tile_blocklinear_kernel(tc, x, weight, bias, out_0, out_1):
             state["codes%d" % i] = prep.tile([P, 1024], U32, name="x_codes", tag="x_codes", align_bytes=64)
             state["scales%d" % i] = prep.tile([P, 1024], U8, name="x_scales", tag="x_scales", align_bytes=64)
 
-        def reorder(i, par, m0, m1, i0, i1, on_scalar=False, on_gpsimd=False):
+        def reorder(i, par, m0, m1, i0, i1, on_scalar=False, on_gpsimd=False, gate=None):
             if on_gpsimd:
                 src = x_raw[i][:].rearrange("p (i par m k) -> p par m i k", par=2, m=8, k=16)
                 dst = state["ord%d" % i][:].rearrange("p (m par i k) -> p par m i k", m=8, par=2, k=16)
                 nc.gpsimd.tensor_scalar(
                     out=dst[:, par, m0:m1, i0:i1, :],
                     in0=src[:, par, m0:m1, i0:i1, :],
-                    scalar1=1.0,
+                    scalar1=1.0 if gate is None else gate[:, 0:1],
                     scalar2=0.0,
                     op0=ALU.mult,
                     op1=ALU.add,
@@ -181,6 +182,18 @@ def tile_blocklinear_kernel(tc, x, weight, bias, out_0, out_1):
                 op=ALU.add,
             )
 
+        def add_bias_sg(i, o0, n_o, b):
+            per_bank = 16 // n_o
+            ms = slice(b * per_bank, (b + 1) * per_bank)
+            raw = rawp.tile([P, 512], F32, name="raw", tag="raw")
+            nc.scalar.copy(out=raw[:], in_=state["acc%d_%d" % (o0, b)][:])
+            nc.gpsimd.tensor_tensor(
+                out=state["y%d_%d" % (i, o0)][:].rearrange("p (o m n) -> p o m n", o=n_o, m=8)[:, :, ms, :],
+                in0=raw[:].rearrange("p (m o n) -> p o m n", m=per_bank, o=n_o),
+                in1=bias_sb[:].rearrange("p (o m n) -> p o m n", o=16, m=8)[:, o0 : o0 + n_o, ms, :],
+                op=ALU.add,
+            )
+
         def store_y(i, o0, n_o):
             nc.sync.dma_start(
                 out=y_rows[i * P : (i + 1) * P, o0 * 256 : (o0 + n_o) * 256], in_=state["y%d_%d" % (i, o0)][:]
@@ -195,6 +208,28 @@ def tile_blocklinear_kernel(tc, x, weight, bias, out_0, out_1):
                 )
             else:
                 nc.scalar.activation(out=y8[:, c0:c1], in_=y[:, c0:c1], func=ACT.Copy, scale=Y_SCALE, saturate=False)
+
+        def cast2(i, o0, base, on_vector):
+            y = state["y%d_%d" % (i, o0)]
+            y8 = state["z%d_%d" % (i, base)]
+            c0 = (o0 - base) * 256
+            if on_vector:
+                nc.vector.tensor_scalar(
+                    out=y8[:, c0 : c0 + 1024], in0=y[:], scalar1=Y_SCALE, scalar2=None, op0=ALU.mult, saturate=False
+                )
+            else:
+                nc.scalar.activation(out=y8[:, c0 : c0 + 1024], in_=y[:], func=ACT.Copy, scale=Y_SCALE, saturate=False)
+
+        def cast3(i, o0, c0, c1, on_vector):
+            y = state["y%d_%d" % (i, o0)]
+            y8 = state["z%d_%d" % (i, 0)]
+            d0 = o0 * 256
+            if on_vector:
+                nc.vector.tensor_scalar(
+                    out=y8[:, d0 + c0 : d0 + c1], in0=y[:, c0:c1], scalar1=Y_SCALE, scalar2=None, op0=ALU.mult, saturate=False
+                )
+            else:
+                nc.scalar.activation(out=y8[:, d0 + c0 : d0 + c1], in_=y[:, c0:c1], func=ACT.Copy, scale=Y_SCALE, saturate=False)
 
         def store_y8(i, o0, n_o):
             nc.sync.dma_start(
@@ -274,6 +309,10 @@ def tile_blocklinear_kernel(tc, x, weight, bias, out_0, out_1):
         add_bias(0, 0, 8, 1)
         gather(0, 3, False)
         quantize(0, 3, 4)
+        new_ord(2)
+        gate_h = const.tile([P, 1], F32, name="gate_h")
+        nc.vector.memset(gate_h[:], 1.0)
+        reorder(2, 0, 0, 4, 0, 16, False, True, gate_h)
         multiply(0, 0, 8, 3)
         reorder(1, 0, 0, 8, 0, 16, True)
         reorder(1, 1, 0, 8, 0, 16, True)
@@ -293,6 +332,16 @@ def tile_blocklinear_kernel(tc, x, weight, bias, out_0, out_1):
             if c1 == HALF:
                 store_y8(ci, co, 8)
 
+        def open_gate(k):
+            gate = const.tile([P, 1], F32, name="gate_%s" % k)
+            nc.vector.memset(gate[:], 1.0)
+            return gate
+
+        new_ord(3)
+        RV = []
+        PRE = [0,1,1]
+        POST = [1,1,1]
+        LASTC = [1,1,1,1]
         for i in range(N_TILES):
             nxt = i + 1 < N_TILES
             last = not nxt
@@ -303,7 +352,8 @@ def tile_blocklinear_kernel(tc, x, weight, bias, out_0, out_1):
                 add_bias(i, 0, 8, 0)
                 add_bias(i, 0, 8, 1)
             if last:
-                cast_next(False)
+                for j in range(LASTC[0]):
+                    cast_next(False)
             multiply(i, 8, 8, 0)
             multiply(i, 8, 8, 1)
             if nxt:
@@ -314,13 +364,14 @@ def tile_blocklinear_kernel(tc, x, weight, bias, out_0, out_1):
                 add_bias(i, 0, 8, 3)
                 store_y(i, 0, 8)
             if last:
-                cast_next(False)
+                for j in range(LASTC[1]):
+                    cast_next(False)
             multiply(i, 8, 8, 2)
             multiply(i, 8, 8, 3)
             todo.extend([(i, 0, 0, 1024), (i, 0, 1024, HALF)])
-            if i > 0 and nxt:
-                cast_next(False)
             if nxt:
+                for j in range(PRE[i]):
+                    cast_next(False)
                 for g in range(4):
                     gather(i + 1, g, False)
             new_y(i, 8, 8)
@@ -328,21 +379,40 @@ def tile_blocklinear_kernel(tc, x, weight, bias, out_0, out_1):
             add_bias(i, 8, 8, 1)
             if nxt:
                 quantize(i + 1, 0, 2)
+                if i == 0:
+                    pass
+                if i == 1:
+                    pass
+                if i == 2:
+                    pass
             if last:
-                cast_next(False)
+                for j in range(LASTC[2]):
+                    cast_next(False)
             add_bias(i, 8, 8, 2)
             add_bias(i, 8, 8, 3)
             store_y(i, 8, 8)
             todo.extend([(i, 8, 0, 1024), (i, 8, 1024, HALF)])
             if nxt:
                 quantize(i + 1, 2, 4)
+                if i == 0:
+                    gate = open_gate("b0")
+                    reorder(3, 0, 0, 4, 0, 16, False, True, gate)
+                    reorder(3, 1, 0, 4, 0, 16, False, True, gate)
+                if i == 1:
+                    pass
             if last:
-                cast_next(False)
+                for j in range(LASTC[3]):
+                    cast_next(False)
             if i + 2 < N_TILES:
                 new_prep(i + 2)
-                for par in range(2):
-                    reorder(i + 2, par, 0, 8, 0, 16, True)
-            if i == 2:
-                cast_next(False)
+                if i == 0:
+                    reorder(2, 0, 4, 8, 0, 16, True)
+                    reorder(2, 1, 0, 8, 0, 16, True)
+                if i == 1:
+                    reorder(3, 0, 4, 8, 0, 16, True)
+                    reorder(3, 1, 4, 8, 0, 16, True)
+            if nxt:
+                for j in range(POST[i]):
+                    cast_next(False)
         for j in range(len(todo) - state["cast_done"]):
             cast_next(TAIL_ON_V[j])

@@ -319,6 +319,11 @@ def tile_blocklinear_kernel(tc, x, weight, bias, out_0, out_1):
         add_bias(0, 0, 8, 2)
         add_bias(0, 0, 8, 3)
         store_y(0, 0, 8)
+        VGAP = [1,0,0]
+        SG0 = [0,0,0,0]
+        SG1 = [0,0,0,0]
+        FINE_END = False
+        TAIL = [True, True, False, True, True, False]
 
         todo = []
         state["cast_done"] = 0
@@ -349,7 +354,10 @@ def tile_blocklinear_kernel(tc, x, weight, bias, out_0, out_1):
                 for b in range(4):
                     multiply(i, 0, 8, b)
                 new_y(i, 0, 8)
-                add_bias(i, 0, 8, 0)
+                if SG0[i]:
+                    add_bias_sg(i, 0, 8, 0)
+                else:
+                    add_bias(i, 0, 8, 0)
                 add_bias(i, 0, 8, 1)
             if last:
                 for j in range(LASTC[0]):
@@ -375,9 +383,14 @@ def tile_blocklinear_kernel(tc, x, weight, bias, out_0, out_1):
                 for g in range(4):
                     gather(i + 1, g, False)
             new_y(i, 8, 8)
-            add_bias(i, 8, 8, 0)
+            if SG1[i]:
+                add_bias_sg(i, 8, 8, 0)
+            else:
+                add_bias(i, 8, 8, 0)
             add_bias(i, 8, 8, 1)
             if nxt:
+                for j in range(VGAP[i]):
+                    cast_next(True)
                 quantize(i + 1, 0, 2)
                 if i == 0:
                     pass
@@ -391,7 +404,10 @@ def tile_blocklinear_kernel(tc, x, weight, bias, out_0, out_1):
             add_bias(i, 8, 8, 2)
             add_bias(i, 8, 8, 3)
             store_y(i, 8, 8)
-            todo.extend([(i, 8, 0, 1024), (i, 8, 1024, HALF)])
+            if last and FINE_END:
+                todo.extend([(i, 8, 0, 512), (i, 8, 512, 1024), (i, 8, 1024, 1536), (i, 8, 1536, HALF)])
+            else:
+                todo.extend([(i, 8, 0, 1024), (i, 8, 1024, HALF)])
             if nxt:
                 quantize(i + 1, 2, 4)
                 if i == 0:
@@ -415,4 +431,4 @@ def tile_blocklinear_kernel(tc, x, weight, bias, out_0, out_1):
                 for j in range(POST[i]):
                     cast_next(False)
         for j in range(len(todo) - state["cast_done"]):
-            cast_next(TAIL_ON_V[j])
+            cast_next(TAIL[j])

@@ -13,14 +13,19 @@ ACT = mybir.ActivationFunctionType
 ALU = mybir.AluOpType
 
 P = 128
-TOKENS = 512
+N_TILES = 4
 FEATURES = 4096
-N_TILES = TOKENS // P
-Y_SCALE = 210.0
+BANK = 512
 HALF = 2048
+CHUNK = 1024
+N_CHUNKS = N_TILES * FEATURES // CHUNK
+MOVING = 256
+W_COLUMNS = 512
+W_VALUES = 2048
+PAIR_WORDS = 2 * P
+PAIR_VALUES = 4 * PAIR_WORDS
+Y_SCALE = 210.0
 N_WARM = 4
-N_S_BEFORE = 6
-TAIL_ON_V = [True, True, False, True, True, False, True, True, False, True, True]
 
 FLOPS = 2 * 4096 * 512 * 512
 
@@ -34,11 +39,10 @@ def tile_blocklinear_kernel(tc, x, weight, bias, out_0, out_1):
     with ExitStack() as ctx:
         const = ctx.enter_context(tc.tile_pool(name="const", bufs=1))
         xin = ctx.enter_context(tc.tile_pool(name="xin", bufs=N_TILES))
+        ordp = ctx.enter_context(tc.tile_pool(name="ordp", bufs=N_TILES))
+        outp = ctx.enter_context(tc.tile_pool(name="outp", bufs=2 * N_TILES))
+        out8 = ctx.enter_context(tc.tile_pool(name="out8", bufs=2 * N_TILES))
         prep = ctx.enter_context(tc.tile_pool(name="prep", bufs=2))
-        ordp = ctx.enter_context(tc.tile_pool(name="ordp", bufs=4))
-        rawp = ctx.enter_context(tc.tile_pool(name="rawp", bufs=3))
-        outp = ctx.enter_context(tc.tile_pool(name="outp", bufs=10))
-        out8 = ctx.enter_context(tc.tile_pool(name="out8", bufs=10))
         psum_t = ctx.enter_context(tc.psum_pool(name="psum_t", bufs=4))
         psum_o = ctx.enter_context(tc.psum_pool(name="psum_o", bufs=4))
         ctx.enter_context(tc.manual_schedule())
@@ -47,14 +51,14 @@ def tile_blocklinear_kernel(tc, x, weight, bias, out_0, out_1):
         seed_out = const.tile([P, 1], F32, name="seed_out")
         ident = const.tile([P, P], F32, name="ident")
         ident_bf = const.tile([P, P], BF16, name="ident_bf")
-        warm = const.tile([P, 512], BF16, name="warm")
-        bias_rows = const.tile([P, 512], BF16, name="bias_rows")
+        warm = const.tile([P, BANK], BF16, name="warm")
+        bias_rows = const.tile([P, BANK], BF16, name="bias_rows")
         bias_sb = const.tile([P, FEATURES], BF16, name="bias_sb")
-        w_raw = const.tile([P, 2048], BF16, name="w_raw")
-        w_ord = const.tile([P, 2048], BF16, name="w_ord", align_bytes=64)
-        w_grp = const.tile([P, 2048], BF16, name="w_grp", align_bytes=64)
-        w_codes = const.tile([P, 512], U32, name="w_codes", align_bytes=64)
-        w_scales = const.tile([P, 512], U8, name="w_scales", align_bytes=64)
+        w_raw = const.tile([P, W_VALUES], BF16, name="w_raw")
+        w_ord = const.tile([P, W_VALUES], BF16, name="w_ord", align_bytes=64)
+        w_grp = const.tile([P, W_VALUES], BF16, name="w_grp", align_bytes=64)
+        w_codes = const.tile([P, W_COLUMNS], U32, name="w_codes", align_bytes=64)
+        w_scales = const.tile([P, W_COLUMNS], U8, name="w_scales", align_bytes=64)
 
         nc.vector.memset(bias_rows[:], 0.0)
         nc.vector.memset(warm[:], 0.0)
@@ -68,367 +72,264 @@ def tile_blocklinear_kernel(tc, x, weight, bias, out_0, out_1):
             xt = xin.tile([P, FEATURES], BF16, name="x_raw%d" % i, tag="x_raw")
             x_raw.append(xt)
         w_view = weight.rearrange("o (i par) (ng mm) k -> ng par o i (mm k)", par=2, ng=4, mm=8)
-        bias_flat = bias.rearrange("o m n -> (o m n)")
 
         def load_w(s):
             nc.sync.dma_start(out=w_raw[s:P:8, :].rearrange("p (i f) -> p i f", i=16), in_=w_view[s // 2, s % 2])
 
-        def load_x0(q):
-            nc.sync.dma_start(out=x_raw[0][:, q * HALF : (q + 1) * HALF], in_=x_rows[0:P, q * HALF : (q + 1) * HALF])
-
-        def load_bias():
-            nc.sync.dma_start(out=bias_rows[0:8, :], in_=bias_flat.rearrange("(g c) -> g c", g=8))
+        def load_x0(c_low):
+            cols = slice(0, FEATURES // 2) if c_low else slice(FEATURES // 2, FEATURES)
+            nc.sync.dma_start(out=x_raw[0][:, cols], in_=x_rows[0:P, cols])
 
         load_w(0)
         load_w(1)
-        load_bias()
+        nc.sync.dma_start(out=bias_rows[0:8, :], in_=bias.rearrange("o m n -> (o m n)").rearrange("(r c) -> r c", r=8))
         for s in range(2, 6):
             load_w(s)
-        load_x0(0)
+        load_x0(True)
         load_w(6)
         load_w(7)
-        load_x0(1)
+        load_x0(False)
         for i in range(1, N_TILES):
             nc.sync.dma_start(out=x_raw[i][:], in_=x_rows[i * P : (i + 1) * P, :])
 
-        state = {}
+        x_ord = {}
+        x_grp = {}
+        x_codes = {}
+        x_scales = {}
+        turned = {}
+        acc = {}
+        y = {}
+        y8 = {}
 
         def new_ord(i):
-            state["ord%d" % i] = ordp.tile([P, FEATURES], BF16, name="x_ord", tag="x_ord", align_bytes=64)
+            x_ord[i] = ordp.tile([P, FEATURES], BF16, name="x_ord", tag="x_ord", align_bytes=64)
 
         def new_prep(i):
-            if "ord%d" % i not in state:
-                new_ord(i)
-            state["grp%d" % i] = prep.tile([P, FEATURES], BF16, name="x_grp", tag="x_grp", align_bytes=64)
-            state["codes%d" % i] = prep.tile([P, 1024], U32, name="x_codes", tag="x_codes", align_bytes=64)
-            state["scales%d" % i] = prep.tile([P, 1024], U8, name="x_scales", tag="x_scales", align_bytes=64)
+            x_grp[i] = prep.tile([P, FEATURES], BF16, name="x_grp", tag="x_grp", align_bytes=64)
+            x_codes[i] = prep.tile([P, 4 * PAIR_WORDS], U32, name="x_codes", tag="x_codes", align_bytes=64)
+            x_scales[i] = prep.tile([P, 4 * PAIR_WORDS], U8, name="x_scales", tag="x_scales", align_bytes=64)
 
-        def reorder(i, par, m0, m1, i0, i1, on_scalar=False, on_gpsimd=False, gate=None):
-            if on_gpsimd:
-                src = x_raw[i][:].rearrange("p (i par m k) -> p par m i k", par=2, m=8, k=16)
-                dst = state["ord%d" % i][:].rearrange("p (m par i k) -> p par m i k", m=8, par=2, k=16)
-                nc.gpsimd.tensor_scalar(
-                    out=dst[:, par, m0:m1, i0:i1, :],
-                    in0=src[:, par, m0:m1, i0:i1, :],
-                    scalar1=1.0 if gate is None else gate[:, 0:1],
-                    scalar2=0.0,
-                    op0=ALU.mult,
-                    op1=ALU.add,
-                )
-            elif on_scalar:
-                src = x_raw[i][:].bitcast(F32).rearrange("p (i par m kk) -> p par m i kk", par=2, m=8, kk=8)
-                dst = state["ord%d" % i][:].bitcast(F32).rearrange("p (m par i kk) -> p par m i kk", m=8, par=2, kk=8)
-                nc.scalar.copy(out=dst[:, par, m0:m1, i0:i1, :], in_=src[:, par, m0:m1, i0:i1, :])
-            else:
-                src = x_raw[i][:].rearrange("p (i par m k) -> p par m i k", par=2, m=8, k=16)
-                dst = state["ord%d" % i][:].rearrange("p (m par i k) -> p par m i k", m=8, par=2, k=16)
-                nc.vector.tensor_copy(out=dst[:, par, m0:m1, i0:i1, :], in_=src[:, par, m0:m1, i0:i1, :])
+        def reorder_vector(i, par, m0, m1, i0, i1):
+            src = x_raw[i][:].rearrange("p (i par m k) -> p par m i k", par=2, m=8, k=16)
+            dst = x_ord[i][:].rearrange("p (m par i k) -> p par m i k", m=8, par=2, k=16)
+            nc.vector.tensor_copy(out=dst[:, par, m0:m1, i0:i1, :], in_=src[:, par, m0:m1, i0:i1, :])
+
+        def reorder_scalar(i, par, m0, m1):
+            src = x_raw[i][:].bitcast(F32).rearrange("p (i par m kk) -> p par m i kk", par=2, m=8, kk=8)
+            dst = x_ord[i][:].bitcast(F32).rearrange("p (m par i kk) -> p par m i kk", m=8, par=2, kk=8)
+            nc.scalar.copy(out=dst[:, par, m0:m1, :, :], in_=src[:, par, m0:m1, :, :])
+
+        def reorder_gpsimd(i, par, m0, m1, gate):
+            src = x_raw[i][:].rearrange("p (i par m k) -> p par m i k", par=2, m=8, k=16)
+            dst = x_ord[i][:].rearrange("p (m par i k) -> p par m i k", m=8, par=2, k=16)
+            nc.gpsimd.tensor_scalar(
+                out=dst[:, par, m0:m1, :, :],
+                in0=src[:, par, m0:m1, :, :],
+                scalar1=gate[:, 0:1],
+                scalar2=0.0,
+                op0=ALU.mult,
+                op1=ALU.add,
+            )
+
+        def open_gate(name):
+            gate = const.tile([P, 1], F32, name=name)
+            nc.vector.memset(gate[:], 1.0)
+            return gate
 
         def turn(i, g):
-            tp = psum_t.tile([P, 512], F32, name="tp", tag="tp")
-            words = state["ord%d" % i][:].bitcast(F32)
+            tp = psum_t.tile([P, BANK], F32, name="tp", tag="tp")
+            words = x_ord[i][:].bitcast(F32)
             for s in range(4):
                 blk = 4 * g + s
                 nc.tensor.transpose(tp[:, s * P : (s + 1) * P], words[:, blk * P : (blk + 1) * P], ident[:])
-            state["tp%d_%d" % (i, g)] = tp
+            turned[(i, g)] = tp
 
-        def gather(i, g, on_vector):
-            tp = state["tp%d_%d" % (i, g)]
-            dst = state["grp%d" % i][:].bitcast(F32)[:, g * 512 : (g + 1) * 512]
-            dst = dst.rearrange("p (m t par) -> p m t par", m=2, par=2)
-            src = tp[:].rearrange("p (m par t) -> p m t par", m=2, par=2)
-            if on_vector:
-                nc.vector.tensor_copy(out=dst, in_=src)
-            else:
-                nc.scalar.copy(out=dst, in_=src)
+        def gather(i, g):
+            dst = x_grp[i][:].bitcast(F32)[:, g * BANK : (g + 1) * BANK]
+            nc.scalar.copy(
+                out=dst.rearrange("p (m t par) -> p m t par", m=2, par=2),
+                in_=turned[(i, g)][:].rearrange("p (m par t) -> p m t par", m=2, par=2),
+            )
 
         def quantize(i, g0, g1):
             nc.vector.quantize_mx(
-                out=state["codes%d" % i][:, g0 * 256 : g1 * 256].bitcast(FP8X4),
-                scales=state["scales%d" % i][:, g0 * 256 : g1 * 256],
-                in_=state["grp%d" % i][:, g0 * 1024 : g1 * 1024],
+                out=x_codes[i][:, g0 * PAIR_WORDS : g1 * PAIR_WORDS].bitcast(FP8X4),
+                scales=x_scales[i][:, g0 * PAIR_WORDS : g1 * PAIR_WORDS],
+                in_=x_grp[i][:, g0 * PAIR_VALUES : g1 * PAIR_VALUES],
             )
 
-        def multiply(i, o0, n_o, b):
-            width = 32 * n_o
-            per_bank = 512 // width
-            acc = psum_o.tile([P, 512], F32, name="acc", tag="acc")
-            for mm in range(per_bank):
-                m = b * per_bank + mm
+        def multiply(i, h, b):
+            bank = psum_o.tile([P, BANK], F32, name="acc", tag="acc")
+            for s in range(2):
+                m = 2 * b + s
                 nc.tensor.matmul_mx(
-                    out=acc[:, mm * width : (mm + 1) * width],
-                    lhsT=state["codes%d" % i][:, m * P : (m + 1) * P].bitcast(FP8X4),
-                    lhsT_scale=state["scales%d" % i][:, m * P : (m + 1) * P],
-                    rhs=w_codes[:, o0 * 32 : o0 * 32 + width].bitcast(FP8X4),
-                    rhs_scale=w_scales[:, o0 * 32 : o0 * 32 + width],
+                    out=bank[:, s * MOVING : (s + 1) * MOVING],
+                    lhsT=x_codes[i][:, m * P : (m + 1) * P].bitcast(FP8X4),
+                    lhsT_scale=x_scales[i][:, m * P : (m + 1) * P],
+                    rhs=w_codes[:, h * MOVING : (h + 1) * MOVING].bitcast(FP8X4),
+                    rhs_scale=w_scales[:, h * MOVING : (h + 1) * MOVING],
                     start=True,
                     stop=True,
                 )
-            state["acc%d_%d" % (o0, b)] = acc
+            acc[(h, b)] = bank
 
-        def new_y(i, o0, n_o):
-            state["y%d_%d" % (i, o0)] = outp.tile([P, n_o * 256], F32, name="y", tag="y")
+        def new_y(i, h):
+            y[(i, h)] = outp.tile([P, HALF], F32, name="y", tag="y")
 
-        def new_y8(i, o0, n_o):
-            state["z%d_%d" % (i, o0)] = out8.tile([P, n_o * 256], FP8, name="y8", tag="y8")
-
-        def add_bias(i, o0, n_o, b):
-            per_bank = 16 // n_o
-            ms = slice(b * per_bank, (b + 1) * per_bank)
+        def add_bias(i, h, b):
+            ms = slice(2 * b, 2 * b + 2)
             nc.vector.tensor_tensor(
-                out=state["y%d_%d" % (i, o0)][:].rearrange("p (o m n) -> p o m n", o=n_o, m=8)[:, :, ms, :],
-                in0=state["acc%d_%d" % (o0, b)][:].rearrange("p (m o n) -> p o m n", m=per_bank, o=n_o),
-                in1=bias_sb[:].rearrange("p (o m n) -> p o m n", o=16, m=8)[:, o0 : o0 + n_o, ms, :],
+                out=y[(i, h)][:].rearrange("p (o m n) -> p o m n", o=8, m=8)[:, :, ms, :],
+                in0=acc[(h, b)][:].rearrange("p (m o n) -> p o m n", m=2, o=8),
+                in1=bias_sb[:].rearrange("p (o m n) -> p o m n", o=16, m=8)[:, 8 * h : 8 * h + 8, ms, :],
                 op=ALU.add,
             )
 
-        def add_bias_sg(i, o0, n_o, b):
-            per_bank = 16 // n_o
-            ms = slice(b * per_bank, (b + 1) * per_bank)
-            raw = rawp.tile([P, 512], F32, name="raw", tag="raw")
-            nc.scalar.copy(out=raw[:], in_=state["acc%d_%d" % (o0, b)][:])
-            nc.gpsimd.tensor_tensor(
-                out=state["y%d_%d" % (i, o0)][:].rearrange("p (o m n) -> p o m n", o=n_o, m=8)[:, :, ms, :],
-                in0=raw[:].rearrange("p (m o n) -> p o m n", m=per_bank, o=n_o),
-                in1=bias_sb[:].rearrange("p (o m n) -> p o m n", o=16, m=8)[:, o0 : o0 + n_o, ms, :],
-                op=ALU.add,
-            )
+        def store_y(i, h):
+            nc.sync.dma_start(out=y_rows[i * P : (i + 1) * P, h * HALF : (h + 1) * HALF], in_=y[(i, h)][:])
 
-        def store_y(i, o0, n_o):
-            nc.sync.dma_start(
-                out=y_rows[i * P : (i + 1) * P, o0 * 256 : (o0 + n_o) * 256], in_=state["y%d_%d" % (i, o0)][:]
-            )
+        n_cast = [0]
 
-        def cast(i, o0, c0, c1, on_vector):
-            y = state["y%d_%d" % (i, o0)]
-            y8 = state["z%d_%d" % (i, o0)]
+        def cast_next(on_vector):
+            q = n_cast[0]
+            n_cast[0] = q + 1
+            i, h, second = q // 4, (q // 2) % 2, q % 2
+            cols = slice(second * CHUNK, (second + 1) * CHUNK)
+            if not second:
+                y8[(i, h)] = out8.tile([P, HALF], FP8, name="y8", tag="y8")
+            dst = y8[(i, h)][:, cols]
+            src = y[(i, h)][:, cols]
             if on_vector:
-                nc.vector.tensor_scalar(
-                    out=y8[:, c0:c1], in0=y[:, c0:c1], scalar1=Y_SCALE, scalar2=None, op0=ALU.mult, saturate=False
+                nc.vector.tensor_scalar(out=dst, in0=src, scalar1=Y_SCALE, scalar2=None, op0=ALU.mult, saturate=False)
+            else:
+                nc.scalar.activation(out=dst, in_=src, func=ACT.Copy, scale=Y_SCALE, saturate=False)
+            if second:
+                nc.sync.dma_start(
+                    out=y8_rows[i * P : (i + 1) * P, h * HALF : (h + 1) * HALF], in_=y8[(i, h)][:].bitcast(U8)
                 )
-            else:
-                nc.scalar.activation(out=y8[:, c0:c1], in_=y[:, c0:c1], func=ACT.Copy, scale=Y_SCALE, saturate=False)
-
-        def cast2(i, o0, base, on_vector):
-            y = state["y%d_%d" % (i, o0)]
-            y8 = state["z%d_%d" % (i, base)]
-            c0 = (o0 - base) * 256
-            if on_vector:
-                nc.vector.tensor_scalar(
-                    out=y8[:, c0 : c0 + 1024], in0=y[:], scalar1=Y_SCALE, scalar2=None, op0=ALU.mult, saturate=False
-                )
-            else:
-                nc.scalar.activation(out=y8[:, c0 : c0 + 1024], in_=y[:], func=ACT.Copy, scale=Y_SCALE, saturate=False)
-
-        def cast3(i, o0, c0, c1, on_vector):
-            y = state["y%d_%d" % (i, o0)]
-            y8 = state["z%d_%d" % (i, 0)]
-            d0 = o0 * 256
-            if on_vector:
-                nc.vector.tensor_scalar(
-                    out=y8[:, d0 + c0 : d0 + c1], in0=y[:, c0:c1], scalar1=Y_SCALE, scalar2=None, op0=ALU.mult, saturate=False
-                )
-            else:
-                nc.scalar.activation(out=y8[:, d0 + c0 : d0 + c1], in_=y[:, c0:c1], func=ACT.Copy, scale=Y_SCALE, saturate=False)
-
-        def store_y8(i, o0, n_o):
-            nc.sync.dma_start(
-                out=y8_rows[i * P : (i + 1) * P, o0 * 256 : (o0 + n_o) * 256],
-                in_=state["z%d_%d" % (i, o0)][:].bitcast(U8),
-            )
-
-        w_src = w_raw[:].rearrange("p (i mm k) -> p mm i k", i=16, mm=8)
-        w_dst = w_ord[:].rearrange("p (mm i k) -> p mm i k", mm=8, i=16)
-        w_words = w_ord[:].bitcast(F32)
-        w_grp_view = w_grp[:].bitcast(F32).rearrange("p (q mm par) -> p q mm par", mm=8, par=2)
-
-        def w_reorder(bank):
-            nc.vector.tensor_copy(out=w_dst[:, 4 * bank : 4 * bank + 4], in_=w_src[:, 4 * bank : 4 * bank + 4])
-
-        def w_turn(bank):
-            tw = psum_t.tile([P, 512], F32, name="tw", tag="tp")
-            for s in range(4):
-                mm = 4 * bank + s
-                nc.tensor.transpose(tw[:, s * P : (s + 1) * P], w_words[:, mm * P : (mm + 1) * P], ident[:])
-            state["tw%d" % bank] = tw
-
-        def w_gather(bank, on_vector):
-            tw_view = state["tw%d" % bank][:].rearrange("p (mm q par) -> p q mm par", mm=4, par=2)
-            if on_vector:
-                nc.vector.tensor_copy(out=w_grp_view[:, :, 4 * bank : 4 * bank + 4, :], in_=tw_view)
-            else:
-                nc.scalar.copy(out=w_grp_view[:, :, 4 * bank : 4 * bank + 4, :], in_=tw_view)
-
-        def w_quantize():
-            nc.vector.quantize_mx(out=w_codes[:].bitcast(FP8X4), scales=w_scales[:], in_=w_grp[:])
 
         for j in range(N_WARM):
-            pw = psum_t.tile([P, 512], F32, name="pw", tag="tp")
+            pw = psum_t.tile([P, BANK], F32, name="pw", tag="tp")
             nc.tensor.matmul(out=pw[:], lhsT=warm[:, 0:P], rhs=warm[:], start=True, stop=True)
         for j in range(4):
-            pb = psum_o.tile([P, 1024], BF16, name="pb", tag="acc")
-            for h in range(2):
-                g = 2 * j + h
+            pb = psum_o.tile([P, 2 * BANK], BF16, name="pb", tag="acc")
+            for s in range(2):
+                r = 2 * j + s
                 nc.tensor.matmul(
-                    out=pb[:, h * 512 : (h + 1) * 512],
-                    lhsT=ident_bf[:, g : g + 1].to_broadcast([P, P]),
+                    out=pb[:, s * BANK : (s + 1) * BANK],
+                    lhsT=ident_bf[:, r : r + 1].to_broadcast([P, P]),
                     rhs=bias_rows[:],
                     start=True,
                     stop=True,
                 )
             if j % 2 == 0:
-                nc.vector.tensor_copy(out=bias_sb[:, j * 1024 : (j + 1) * 1024], in_=pb[:])
+                nc.vector.tensor_copy(out=bias_sb[:, j * 2 * BANK : (j + 1) * 2 * BANK], in_=pb[:])
             else:
-                nc.scalar.copy(out=bias_sb[:, j * 1024 : (j + 1) * 1024], in_=pb[:])
+                nc.scalar.copy(out=bias_sb[:, j * 2 * BANK : (j + 1) * 2 * BANK], in_=pb[:])
+
+        new_ord(0)
         new_prep(0)
         for par in range(2):
-            reorder(0, par, 0, 8, 0, 8)
-        for bank in range(2):
-            w_reorder(bank)
-            w_turn(bank)
-        for mh in range(2):
+            reorder_vector(0, par, 0, 8, 0, 8)
+        w_src = w_raw[:].rearrange("p (i mm k) -> p mm i k", i=16, mm=8)
+        w_dst = w_ord[:].rearrange("p (mm i k) -> p mm i k", mm=8, i=16)
+        w_words = w_ord[:].bitcast(F32)
+        w_turned = []
+        for b in range(2):
+            nc.vector.tensor_copy(out=w_dst[:, 4 * b : 4 * b + 4], in_=w_src[:, 4 * b : 4 * b + 4])
+            tw = psum_t.tile([P, BANK], F32, name="tw", tag="tp")
+            for s in range(4):
+                mm = 4 * b + s
+                nc.tensor.transpose(tw[:, s * P : (s + 1) * P], w_words[:, mm * P : (mm + 1) * P], ident[:])
+            w_turned.append(tw)
+        for m0 in (0, 4):
             for par in range(2):
-                reorder(0, par, 4 * mh, 4 * mh + 4, 8, 16)
-        w_gather(0, False)
-        w_gather(1, False)
+                reorder_vector(0, par, m0, m0 + 4, 8, 16)
+        w_grp_view = w_grp[:].bitcast(F32).rearrange("p (q mm par) -> p q mm par", mm=8, par=2)
+        for b in range(2):
+            nc.scalar.copy(
+                out=w_grp_view[:, :, 4 * b : 4 * b + 4, :],
+                in_=w_turned[b][:].rearrange("p (mm q par) -> p q mm par", mm=4, par=2),
+            )
         for g in range(4):
             turn(0, g)
-        w_quantize()
-        new_y(0, 0, 8)
+        nc.vector.quantize_mx(out=w_codes[:].bitcast(FP8X4), scales=w_scales[:], in_=w_grp[:])
+        new_y(0, 0)
+        new_ord(1)
         new_prep(1)
-        gather(0, 0, False)
-        quantize(0, 0, 1)
-        multiply(0, 0, 8, 0)
-        gather(0, 1, False)
-        quantize(0, 1, 2)
-        multiply(0, 0, 8, 1)
-        add_bias(0, 0, 8, 0)
-        gather(0, 2, False)
-        quantize(0, 2, 3)
-        multiply(0, 0, 8, 2)
-        add_bias(0, 0, 8, 1)
-        gather(0, 3, False)
-        quantize(0, 3, 4)
         new_ord(2)
-        gate_h = const.tile([P, 1], F32, name="gate_h")
-        nc.vector.memset(gate_h[:], 1.0)
-        reorder(2, 0, 0, 4, 0, 16, False, True, gate_h)
-        multiply(0, 0, 8, 3)
-        reorder(1, 0, 0, 8, 0, 16, True)
-        reorder(1, 1, 0, 8, 0, 16, True)
-        add_bias(0, 0, 8, 2)
-        add_bias(0, 0, 8, 3)
-        store_y(0, 0, 8)
-        VGAP = [1,0,0]
-        SG0 = [0,0,0,0]
-        SG1 = [0,0,0,0]
-        FINE_END = False
-        TAIL = [True, True, False, True, True, False]
-
-        todo = []
-        state["cast_done"] = 0
-
-        def cast_next(on_vector):
-            ci, co, c0, c1 = todo[state["cast_done"]]
-            state["cast_done"] = state["cast_done"] + 1
-            if c0 == 0:
-                new_y8(ci, co, 8)
-            cast(ci, co, c0, c1, on_vector)
-            if c1 == HALF:
-                store_y8(ci, co, 8)
-
-        def open_gate(k):
-            gate = const.tile([P, 1], F32, name="gate_%s" % k)
-            nc.vector.memset(gate[:], 1.0)
-            return gate
+        for g in range(4):
+            gather(0, g)
+            quantize(0, g, g + 1)
+            if g == 3:
+                reorder_gpsimd(2, 0, 0, 4, open_gate("gate_a"))
+            multiply(0, 0, g)
+            if g > 0:
+                add_bias(0, 0, g - 1)
+        for par in range(2):
+            reorder_scalar(1, par, 0, 8)
+        add_bias(0, 0, 3)
+        store_y(0, 0)
 
         new_ord(3)
-        RV = []
-        PRE = [0,1,1]
-        POST = [1,1,1]
-        LASTC = [1,1,1,1]
         for i in range(N_TILES):
-            nxt = i + 1 < N_TILES
-            last = not nxt
+            more = i + 1 < N_TILES
             if i > 0:
                 for b in range(4):
-                    multiply(i, 0, 8, b)
-                new_y(i, 0, 8)
-                if SG0[i]:
-                    add_bias_sg(i, 0, 8, 0)
-                else:
-                    add_bias(i, 0, 8, 0)
-                add_bias(i, 0, 8, 1)
-            if last:
-                for j in range(LASTC[0]):
-                    cast_next(False)
-            multiply(i, 8, 8, 0)
-            multiply(i, 8, 8, 1)
-            if nxt:
+                    multiply(i, 0, b)
+                new_y(i, 0)
+                add_bias(i, 0, 0)
+                add_bias(i, 0, 1)
+            if not more:
+                cast_next(False)
+            multiply(i, 1, 0)
+            multiply(i, 1, 1)
+            if more:
                 for g in range(4):
                     turn(i + 1, g)
             if i > 0:
-                add_bias(i, 0, 8, 2)
-                add_bias(i, 0, 8, 3)
-                store_y(i, 0, 8)
-            if last:
-                for j in range(LASTC[1]):
-                    cast_next(False)
-            multiply(i, 8, 8, 2)
-            multiply(i, 8, 8, 3)
-            todo.extend([(i, 0, 0, 1024), (i, 0, 1024, HALF)])
-            if nxt:
-                for j in range(PRE[i]):
+                add_bias(i, 0, 2)
+                add_bias(i, 0, 3)
+                store_y(i, 0)
+            if not more:
+                cast_next(False)
+            multiply(i, 1, 2)
+            multiply(i, 1, 3)
+            if more:
+                if i > 0:
                     cast_next(False)
                 for g in range(4):
-                    gather(i + 1, g, False)
-            new_y(i, 8, 8)
-            if SG1[i]:
-                add_bias_sg(i, 8, 8, 0)
-            else:
-                add_bias(i, 8, 8, 0)
-            add_bias(i, 8, 8, 1)
-            if nxt:
-                for j in range(VGAP[i]):
-                    cast_next(True)
+                    gather(i + 1, g)
+            new_y(i, 1)
+            add_bias(i, 1, 0)
+            add_bias(i, 1, 1)
+            if i == 0:
+                cast_next(True)
+            if more:
                 quantize(i + 1, 0, 2)
-                if i == 0:
-                    pass
-                if i == 1:
-                    pass
-                if i == 2:
-                    pass
-            if last:
-                for j in range(LASTC[2]):
-                    cast_next(False)
-            add_bias(i, 8, 8, 2)
-            add_bias(i, 8, 8, 3)
-            store_y(i, 8, 8)
-            if last and FINE_END:
-                todo.extend([(i, 8, 0, 512), (i, 8, 512, 1024), (i, 8, 1024, 1536), (i, 8, 1536, HALF)])
             else:
-                todo.extend([(i, 8, 0, 1024), (i, 8, 1024, HALF)])
-            if nxt:
+                cast_next(False)
+            add_bias(i, 1, 2)
+            add_bias(i, 1, 3)
+            store_y(i, 1)
+            if more:
                 quantize(i + 1, 2, 4)
-                if i == 0:
-                    gate = open_gate("b0")
-                    reorder(3, 0, 0, 4, 0, 16, False, True, gate)
-                    reorder(3, 1, 0, 4, 0, 16, False, True, gate)
-                if i == 1:
-                    pass
-            if last:
-                for j in range(LASTC[3]):
-                    cast_next(False)
+            else:
+                cast_next(False)
+            if i == 0:
+                gate = open_gate("gate_b")
+                for par in range(2):
+                    reorder_gpsimd(3, par, 0, 4, gate)
             if i + 2 < N_TILES:
                 new_prep(i + 2)
                 if i == 0:
-                    reorder(2, 0, 4, 8, 0, 16, True)
-                    reorder(2, 1, 0, 8, 0, 16, True)
-                if i == 1:
-                    reorder(3, 0, 4, 8, 0, 16, True)
-                    reorder(3, 1, 4, 8, 0, 16, True)
-            if nxt:
-                for j in range(POST[i]):
-                    cast_next(False)
-        for j in range(len(todo) - state["cast_done"]):
-            cast_next(TAIL[j])
+                    reorder_scalar(2, 0, 4, 8)
+                    reorder_scalar(2, 1, 0, 8)
+                else:
+                    for par in range(2):
+                        reorder_scalar(3, par, 4, 8)
+            if more:
+                cast_next(False)
+
+        for j in range(N_CHUNKS - n_cast[0]):
+            cast_next(j % 3 != 2)

@@ -39,10 +39,10 @@ def tile_blocklinear_kernel(tc, x, weight, bias, out_0, out_1):
     with ExitStack() as ctx:
         const = ctx.enter_context(tc.tile_pool(name="const", bufs=1))
         xin = ctx.enter_context(tc.tile_pool(name="xin", bufs=N_TILES))
+        prep = ctx.enter_context(tc.tile_pool(name="prep", bufs=2))
         ordp = ctx.enter_context(tc.tile_pool(name="ordp", bufs=N_TILES))
         outp = ctx.enter_context(tc.tile_pool(name="outp", bufs=2 * N_TILES))
         out8 = ctx.enter_context(tc.tile_pool(name="out8", bufs=2 * N_TILES))
-        prep = ctx.enter_context(tc.tile_pool(name="prep", bufs=2))
         psum_t = ctx.enter_context(tc.psum_pool(name="psum_t", bufs=4))
         psum_o = ctx.enter_context(tc.psum_pool(name="psum_o", bufs=4))
         ctx.enter_context(tc.manual_schedule())

from contextlib import ExitStack

import concourse.mybir as mybir
from concourse.masks import make_identity

F32 = mybir.dt.float32
BF16 = mybir.dt.bfloat16
U32 = mybir.dt.uint32
U8 = mybir.dt.uint8
FP8X4 = mybir.dt.float8_e4m3fn_x4
FP8 = mybir.dt.float8_e4m3fn
ACT = mybir.ActivationFunctionType
ALU = mybir.AluOpType

P = 128
N_TILES = 4
FEATURES = 4096
BANK = 512
HALF = 2048
CHUNK = 1024
N_CHUNKS = N_TILES * FEATURES // CHUNK
MOVING = 256
W_COLUMNS = 512
W_VALUES = 2048
PAIR_WORDS = 2 * P
PAIR_VALUES = 4 * PAIR_WORDS
Y_SCALE = 210.0
N_WARM = 4

FLOPS = 2 * 4096 * 512 * 512


def tile_blocklinear_kernel(tc, x, weight, bias, out_0, out_1):
    nc = tc.nc
    x_rows = x.flatten_outer_dims()
    y_rows = out_0.flatten_outer_dims()
    y8_rows = out_1.flatten_outer_dims()

    with ExitStack() as ctx:
        const = ctx.enter_context(tc.tile_pool(name="const", bufs=1))
        xin = ctx.enter_context(tc.tile_pool(name="xin", bufs=N_TILES))
        prep = ctx.enter_context(tc.tile_pool(name="prep", bufs=2))
        ordp = ctx.enter_context(tc.tile_pool(name="ordp", bufs=N_TILES))
        outp = ctx.enter_context(tc.tile_pool(name="outp", bufs=2 * N_TILES))
        out8 = ctx.enter_context(tc.tile_pool(name="out8", bufs=2 * N_TILES))
        psum_t = ctx.enter_context(tc.psum_pool(name="psum_t", bufs=4))
        psum_o = ctx.enter_context(tc.psum_pool(name="psum_o", bufs=4))
        ctx.enter_context(tc.manual_schedule())

        seed = const.tile([P, 1], F32, name="seed")
        seed_out = const.tile([P, 1], F32, name="seed_out")
        ident = const.tile([P, P], F32, name="ident")
        ident_bf = const.tile([P, P], BF16, name="ident_bf")
        warm = const.tile([P, BANK], BF16, name="warm")
        bias_rows = const.tile([P, BANK], BF16, name="bias_rows")
        bias_sb = const.tile([P, FEATURES], BF16, name="bias_sb")
        w_raw = const.tile([P, W_VALUES], BF16, name="w_raw")
        w_ord = const.tile([P, W_VALUES], BF16, name="w_ord", align_bytes=64)
        w_grp = const.tile([P, W_VALUES], BF16, name="w_grp", align_bytes=64)
        w_codes = const.tile([P, W_COLUMNS], U32, name="w_codes", align_bytes=64)
        w_scales = const.tile([P, W_COLUMNS], U8, name="w_scales", align_bytes=64)

        nc.vector.memset(bias_rows[:], 0.0)
        nc.vector.memset(warm[:], 0.0)
        nc.vector.memset(seed[:], 0.0)
        nc.scalar.activation(out=seed_out[:], in_=seed[:], func=ACT.Copy, scale=1.0)
        make_identity(nc, ident_bf[:])
        make_identity(nc, ident[:])

        x_raw = []
        for i in range(N_TILES):
            xt = xin.tile([P, FEATURES], BF16, name="x_raw%d" % i, tag="x_raw")
            x_raw.append(xt)
        w_view = weight.rearrange("o (i par) (ng mm) k -> ng par o i (mm k)", par=2, ng=4, mm=8)

        def load_w(s):
            nc.sync.dma_start(out=w_raw[s:P:8, :].rearrange("p (i f) -> p i f", i=16), in_=w_view[s // 2, s % 2])

        def load_x0(c_low):
            cols = slice(0, FEATURES // 2) if c_low else slice(FEATURES // 2, FEATURES)
            nc.sync.dma_start(out=x_raw[0][:, cols], in_=x_rows[0:P, cols])

        load_w(0)
        load_w(1)
        nc.sync.dma_start(out=bias_rows[0:8, :], in_=bias.rearrange("o m n -> (o m n)").rearrange("(r c) -> r c", r=8))
        for s in range(2, 6):
            load_w(s)
        load_x0(True)
        load_w(6)
        load_w(7)
        load_x0(False)
        for i in range(1, N_TILES):
            nc.sync.dma_start(out=x_raw[i][:], in_=x_rows[i * P : (i + 1) * P, :])

        x_ord = {}
        x_grp = {}
        x_codes = {}
        x_scales = {}
        turned = {}
        acc = {}
        y = {}
        y8 = {}

        def new_ord(i):
            x_ord[i] = ordp.tile([P, FEATURES], BF16, name="x_ord", tag="x_ord", align_bytes=64)

        def new_prep(i):
            x_grp[i] = prep.tile([P, FEATURES], BF16, name="x_grp", tag="x_grp", align_bytes=64)
            x_codes[i] = prep.tile([P, 4 * PAIR_WORDS], U32, name="x_codes", tag="x_codes", align_bytes=64)
            x_scales[i] = prep.tile([P, 4 * PAIR_WORDS], U8, name="x_scales", tag="x_scales", align_bytes=64)

        def reorder_vector(i, par, m0, m1, i0, i1):
            src = x_raw[i][:].rearrange("p (i par m k) -> p par m i k", par=2, m=8, k=16)
            dst = x_ord[i][:].rearrange("p (m par i k) -> p par m i k", m=8, par=2, k=16)
            nc.vector.tensor_copy(out=dst[:, par, m0:m1, i0:i1, :], in_=src[:, par, m0:m1, i0:i1, :])

        def reorder_scalar(i, par, m0, m1):
            src = x_raw[i][:].bitcast(F32).rearrange("p (i par m kk) -> p par m i kk", par=2, m=8, kk=8)
            dst = x_ord[i][:].bitcast(F32).rearrange("p (m par i kk) -> p par m i kk", m=8, par=2, kk=8)
            nc.scalar.copy(out=dst[:, par, m0:m1, :, :], in_=src[:, par, m0:m1, :, :])

        def reorder_gpsimd(i, par, m0, m1, gate):
            src = x_raw[i][:].rearrange("p (i par m k) -> p par m i k", par=2, m=8, k=16)
            dst = x_ord[i][:].rearrange("p (m par i k) -> p par m i k", m=8, par=2, k=16)
            nc.gpsimd.tensor_scalar(
                out=dst[:, par, m0:m1, :, :],
                in0=src[:, par, m0:m1, :, :],
                scalar1=gate[:, 0:1],
                scalar2=0.0,
                op0=ALU.mult,
                op1=ALU.add,
            )

        def open_gate(name):
            gate = const.tile([P, 1], F32, name=name)
            nc.vector.memset(gate[:], 1.0)
            return gate

        def turn(i, g):
            tp = psum_t.tile([P, BANK], F32, name="tp", tag="tp")
            words = x_ord[i][:].bitcast(F32)
            for s in range(4):
                blk = 4 * g + s
                nc.tensor.transpose(tp[:, s * P : (s + 1) * P], words[:, blk * P : (blk + 1) * P], ident[:])
            turned[(i, g)] = tp

        def gather(i, g):
            dst = x_grp[i][:].bitcast(F32)[:, g * BANK : (g + 1) * BANK]
            nc.scalar.copy(
                out=dst.rearrange("p (m t par) -> p m t par", m=2, par=2),
                in_=turned[(i, g)][:].rearrange("p (m par t) -> p m t par", m=2, par=2),
            )

        def quantize(i, g0, g1):
            nc.vector.quantize_mx(
                out=x_codes[i][:, g0 * PAIR_WORDS : g1 * PAIR_WORDS].bitcast(FP8X4),
                scales=x_scales[i][:, g0 * PAIR_WORDS : g1 * PAIR_WORDS],
                in_=x_grp[i][:, g0 * PAIR_VALUES : g1 * PAIR_VALUES],
            )

        def multiply(i, h, b):
            bank = psum_o.tile([P, BANK], F32, name="acc", tag="acc")
            for s in range(2):
                m = 2 * b + s
                nc.tensor.matmul_mx(
                    out=bank[:, s * MOVING : (s + 1) * MOVING],
                    lhsT=x_codes[i][:, m * P : (m + 1) * P].bitcast(FP8X4),
                    lhsT_scale=x_scales[i][:, m * P : (m + 1) * P],
                    rhs=w_codes[:, h * MOVING : (h + 1) * MOVING].bitcast(FP8X4),
                    rhs_scale=w_scales[:, h * MOVING : (h + 1) * MOVING],
                    start=True,
                    stop=True,
                )
            acc[(h, b)] = bank

        def new_y(i, h):
            y[(i, h)] = outp.tile([P, HALF], F32, name="y", tag="y")

        def add_bias(i, h, b):
            ms = slice(2 * b, 2 * b + 2)
            nc.vector.tensor_tensor(
                out=y[(i, h)][:].rearrange("p (o m n) -> p o m n", o=8, m=8)[:, :, ms, :],
                in0=acc[(h, b)][:].rearrange("p (m o n) -> p o m n", m=2, o=8),
                in1=bias_sb[:].rearrange("p (o m n) -> p o m n", o=16, m=8)[:, 8 * h : 8 * h + 8, ms, :],
                op=ALU.add,
            )

        def store_y(i, h):
            nc.sync.dma_start(out=y_rows[i * P : (i + 1) * P, h * HALF : (h + 1) * HALF], in_=y[(i, h)][:])

        n_cast = [0]

        def cast_next(on_vector):
            q = n_cast[0]
            n_cast[0] = q + 1
            i, h, second = q // 4, (q // 2) % 2, q % 2
            cols = slice(second * CHUNK, (second + 1) * CHUNK)
            if not second:
                y8[(i, h)] = out8.tile([P, HALF], FP8, name="y8", tag="y8")
            dst = y8[(i, h)][:, cols]
            src = y[(i, h)][:, cols]
            if on_vector:
                nc.vector.tensor_scalar(out=dst, in0=src, scalar1=Y_SCALE, scalar2=None, op0=ALU.mult, saturate=False)
            else:
                nc.scalar.activation(out=dst, in_=src, func=ACT.Copy, scale=Y_SCALE, saturate=False)
            if second:
                nc.sync.dma_start(
                    out=y8_rows[i * P : (i + 1) * P, h * HALF : (h + 1) * HALF], in_=y8[(i, h)][:].bitcast(U8)
                )

        for j in range(N_WARM):
            pw = psum_t.tile([P, BANK], F32, name="pw", tag="tp")
            nc.tensor.matmul(out=pw[:], lhsT=warm[:, 0:P], rhs=warm[:], start=True, stop=True)
        for j in range(4):
            pb = psum_o.tile([P, 2 * BANK], BF16, name="pb", tag="acc")
            for s in range(2):
                r = 2 * j + s
                nc.tensor.matmul(
                    out=pb[:, s * BANK : (s + 1) * BANK],
                    lhsT=ident_bf[:, r : r + 1].to_broadcast([P, P]),
                    rhs=bias_rows[:],
                    start=True,
                    stop=True,
                )
            if j % 2 == 0:
                nc.vector.tensor_copy(out=bias_sb[:, j * 2 * BANK : (j + 1) * 2 * BANK], in_=pb[:])
            else:
                nc.scalar.copy(out=bias_sb[:, j * 2 * BANK : (j + 1) * 2 * BANK], in_=pb[:])

        new_ord(0)
        new_prep(0)
        for par in range(2):
            reorder_vector(0, par, 0, 8, 0, 8)
        w_src = w_raw[:].rearrange("p (i mm k) -> p mm i k", i=16, mm=8)
        w_dst = w_ord[:].rearrange("p (mm i k) -> p mm i k", mm=8, i=16)
        w_words = w_ord[:].bitcast(F32)
        w_turned = []
        for b in range(2):
            nc.vector.tensor_copy(out=w_dst[:, 4 * b : 4 * b + 4], in_=w_src[:, 4 * b : 4 * b + 4])
            tw = psum_t.tile([P, BANK], F32, name="tw", tag="tp")
            for s in range(4):
                mm = 4 * b + s
                nc.tensor.transpose(tw[:, s * P : (s + 1) * P], w_words[:, mm * P : (mm + 1) * P], ident[:])
            w_turned.append(tw)
        for m0 in (0, 4):
            for par in range(2):
                reorder_vector(0, par, m0, m0 + 4, 8, 16)
        w_grp_view = w_grp[:].bitcast(F32).rearrange("p (q mm par) -> p q mm par", mm=8, par=2)
        for b in range(2):
            nc.scalar.copy(
                out=w_grp_view[:, :, 4 * b : 4 * b + 4, :],
                in_=w_turned[b][:].rearrange("p (mm q par) -> p q mm par", mm=4, par=2),
            )
        for g in range(4):
            turn(0, g)
        nc.vector.quantize_mx(out=w_codes[:].bitcast(FP8X4), scales=w_scales[:], in_=w_grp[:])
        new_y(0, 0)
        new_ord(1)
        new_prep(1)
        new_ord(2)
        for g in range(4):
            gather(0, g)
            quantize(0, g, g + 1)
            if g == 3:
                reorder_gpsimd(2, 0, 0, 4, open_gate("gate_a"))
            multiply(0, 0, g)
            if g > 0:
                add_bias(0, 0, g - 1)
        for par in range(2):
            reorder_scalar(1, par, 0, 8)
        add_bias(0, 0, 3)
        store_y(0, 0)

        new_ord(3)
        for i in range(N_TILES):
            more = i + 1 < N_TILES
            if i > 0:
                for b in range(4):
                    multiply(i, 0, b)
                new_y(i, 0)
                add_bias(i, 0, 0)
                add_bias(i, 0, 1)
            if not more:
                cast_next(False)
            multiply(i, 1, 0)
            multiply(i, 1, 1)
            if more:
                for g in range(4):
                    turn(i + 1, g)
            if i > 0:
                add_bias(i, 0, 2)
                add_bias(i, 0, 3)
                store_y(i, 0)
            if not more:
                cast_next(False)
            multiply(i, 1, 2)
            multiply(i, 1, 3)
            if more:
                if i > 0:
                    cast_next(False)
                for g in range(4):
                    gather(i + 1, g)
            new_y(i, 1)
            add_bias(i, 1, 0)
            add_bias(i, 1, 1)
            if i == 0:
                cast_next(True)
            if more:
                quantize(i + 1, 0, 2)
            else:
                cast_next(False)
            add_bias(i, 1, 2)
            add_bias(i, 1, 3)
            store_y(i, 1)
            if more:
                quantize(i + 1, 2, 4)
            else:
                cast_next(False)
            if i == 0:
                gate = open_gate("gate_b")
                for par in range(2):
                    reorder_gpsimd(3, par, 0, 4, gate)
            if i + 2 < N_TILES:
                new_prep(i + 2)
                if i == 0:
                    reorder_scalar(2, 0, 4, 8)
                    reorder_scalar(2, 1, 0, 8)
                else:
                    for par in range(2):
                        reorder_scalar(3, par, 4, 8)
            if more:
                cast_next(False)

        for j in range(N_CHUNKS - n_cast[0]):
            cast_next(j % 3 != 2)
